import numpy as np
import ml_dtypes


def mxq(x, axis, fmt="e4m3"):
    dtype, down = {"e4m3": (ml_dtypes.float8_e4m3fn, 7), "e5m2": (ml_dtypes.float8_e5m2, 14)}[fmt]
    v = np.moveaxis(np.asarray(x, np.float32).astype(ml_dtypes.bfloat16).astype(np.float64), axis, -1)
    blocks = v.reshape(v.shape[:-1] + (-1, 32))
    amax = np.abs(blocks).max(-1, keepdims=True)
    byte = np.maximum(np.where(amax > 0, np.frexp(amax)[1] - 1 + 127, 0) - down, 1)
    scale = np.exp2(byte - 127.0)
    codes = (blocks / scale).astype(np.float32).astype(dtype).astype(np.float64)
    return np.moveaxis((codes * scale).reshape(v.shape), -1, axis)


WIDE = False


def mx_kscale(k):
    if not WIDE:
        return np.ones(k)
    levels = np.array([10, -10, 5, -5, 0])
    a = np.random.permutation(np.resize(levels, k // 512 * 4)).reshape(k // 512, 4)
    idx = np.arange(k)
    return np.exp2(a[idx // 512, idx % 128 // 32])


BF16 = ml_dtypes.bfloat16


def bf(x):
    return np.asarray(x, np.float32).astype(BF16)


def f64(x):
    return np.asarray(x).astype(np.float64)


B, D, U, G, KS = 6144, 1024, 128, 5, 8
GRID_RANGE = (-1.0, 1.0)


def silu(v):
    return v / (1.0 + np.exp(-v))


def setup_inputs():
    s = mx_kscale(D)
    r = s / s.max()
    return {"x": bf(np.random.standard_normal((B, D)) * r),
            "base_weight": bf(np.random.standard_normal((D, U)) / np.sqrt(D) / r[:, None]),
            "spline_weight": bf(np.random.standard_normal((D, U, KS)) / np.sqrt(D))}


def reference(x, base_weight, spline_weight):
    x = f64(x)
    base_out = silu(mxq(x, 1, "e4m3") @ mxq(f64(base_weight), 0, "e4m3"))
    centers = np.linspace(GRID_RANGE[0], GRID_RANGE[1], G)
    dist = np.square(x[..., None] - centers)
    rbf = np.exp(-5.0 * dist)
    rq = mxq(rbf, 1, "e4m3")
    wq = mxq(f64(spline_weight)[:, :, :G], 0, "e4m3")
    spline_out = (rq.transpose(2, 0, 1) @ wq.transpose(2, 0, 1)).sum(0)
    return base_out + spline_out

@@ -1,0 +1,271 @@
+from contextlib import ExitStack
+
+import concourse.mybir as mybir
+from concourse.masks import make_identity
+
+FP8X4 = mybir.dt.float8_e4m3fn_x4
+BF16 = mybir.dt.bfloat16
+F32 = mybir.dt.float32
+U32 = mybir.dt.uint32
+U8 = mybir.dt.uint8
+AF = mybir.ActivationFunctionType
+ALU = mybir.AluOpType
+
+P = 128
+ROWS, FEAT, UNITS = 6144, 1024, 128
+CENTRES = (-1.0, -0.5, 0.0, 0.5, 1.0)
+NG = len(CENTRES)
+MAPS = 1 + NG
+FLOPS = 2 * ROWS * FEAT * UNITS * MAPS
+
+CHUNKS = (1, 1, 2) + (4,) * 10 + (2, 1, 1)
+CMAX = 4
+ACT_SHARE_32 = 7
+W_SLOT = 4
+
+
+def tile_kandense_t_kernel(tc, x, base_weight, spline_weight, out):
+    nc = tc.nc
+    assert sum(CHUNKS) * P == ROWS
+    row0 = [P * sum(CHUNKS[:c]) for c in range(len(CHUNKS))]
+    n_chunks = len(CHUNKS)
+
+    with ExitStack() as ctx:
+        const = ctx.enter_context(tc.tile_pool(name="const", bufs=1))
+        xn_pool = ctx.enter_context(tc.tile_pool(name="xn", bufs=2))
+        xg_pool = ctx.enter_context(tc.tile_pool(name="xg", bufs=2))
+        arg_pool = ctx.enter_context(tc.tile_pool(name="arg", bufs=3))
+        rg_pool = ctx.enter_context(tc.tile_pool(name="rg", bufs=3))
+        cd_pool = ctx.enter_context(tc.tile_pool(name="cd", bufs=2))
+        ep_pool = ctx.enter_context(tc.tile_pool(name="ep", bufs=2))
+        xt_pool = ctx.enter_context(tc.psum_pool(name="xt", bufs=4))
+        acc_pool = ctx.enter_context(tc.psum_pool(name="acc", bufs=2))
+        ctx.enter_context(tc.manual_schedule())
+
+        ident = const.tile([P, P], F32, name="ident")
+        make_identity(nc, ident[:])
+        shift = const.tile([P, 2 * 8], F32, name="shift")
+        for g in range(NG):
+            nc.vector.memset(shift[:, g : g + 1], -CENTRES[g])
+            nc.vector.memset(shift[:, 8 + g : 9 + g], -5.0 * CENTRES[g] * CENTRES[g])
+        warm_in = const.tile([P, 1], F32, name="warm_in")
+        warm_out = const.tile([P, 1], F32, name="warm_out")
+        nc.vector.memset(warm_in[:], 0.0)
+        nc.scalar.activation(out=warm_out[:], in_=warm_in[:], func=AF.Exp)
+
+        wb_raw = const.tile([P, 4, 2 * UNITS], BF16, name="wb_raw")
+        ws_raw = const.tile([P, 4, 2 * UNITS * 8], BF16, name="ws_raw")
+        w_grouped = const.tile([P, MAPS, 2, UNITS, 4], BF16, name="w_grouped", align_bytes=64)
+        w_codes = const.tile([P, MAPS * 2 * UNITS], U32, name="w_codes", align_bytes=64)
+        w_scales = const.tile([P, MAPS * 2 * UNITS], U8, name="w_scales", align_bytes=64)
+
+        st = [dict() for c in range(n_chunks)]
+
+        def load(c):
+            n = CHUNKS[c]
+            xn = xn_pool.tile([P, CMAX, FEAT], BF16, name="xn")
+            st[c]["xn"] = xn
+            nc.sync.dma_start(
+                out=xn[:, :n, :],
+                in_=x[row0[c] : row0[c] + P * n, :].rearrange("(p t) k -> p t k", t=n),
+            )
+
+        def load_weights():
+            nc.sync.dma_start(
+                out=wb_raw[:], in_=base_weight.rearrange("(a p e) c -> p a (e c)", a=4, p=P, e=2)
+            )
+            nc.sync.dma_start(
+                out=ws_raw[:],
+                in_=spline_weight.rearrange("(a p e) c s -> p a (e c s)", a=4, p=P, e=2),
+            )
+
+        def prepare_weights():
+            flat = w_grouped[:].rearrange("p m h c t -> p (m h c t)")
+            for h in range(2):
+                nc.vector.tensor_copy(
+                    out=w_grouped[:, 0, h].rearrange("p c (u e) -> p c u e", u=2),
+                    in_=wb_raw[:, 2 * h : 2 * h + 2, :].rearrange("p u (e c) -> p c u e", e=2),
+                )
+            nc.vector.quantize_mx(
+                out=w_codes[:, 0:256].bitcast(FP8X4), scales=w_scales[:, 0:256], in_=flat[:, 0:1024]
+            )
+            for g in range(NG):
+                for h in range(2):
+                    nc.vector.tensor_copy(
+                        out=w_grouped[:, 1 + g, h].rearrange("p c (u e) -> p c u e", u=2),
+                        in_=ws_raw[:, 2 * h : 2 * h + 2, :].rearrange(
+                            "p u (e c s) -> p c u e s", e=2, s=8
+                        )[:, :, :, :, g],
+                    )
+            nc.vector.quantize_mx(
+                out=w_codes[:, 256:1280].bitcast(FP8X4),
+                scales=w_scales[:, 256:1280],
+                in_=flat[:, 1024:5120],
+            )
+            nc.vector.quantize_mx(
+                out=w_codes[:, 1280:1536].bitcast(FP8X4),
+                scales=w_scales[:, 1280:1536],
+                in_=flat[:, 5120:6144],
+            )
+
+        def transposes(c):
+            words = st[c]["xn"][:].bitcast(F32)
+            st[c]["xt"] = []
+            for t in range(CHUNKS[c]):
+                xt = xt_pool.tile([P, 512], F32, name="xt")
+                st[c]["xt"].append(xt)
+                for j in range(4):
+                    h, u = divmod(j, 2)
+                    pos = 2 * u + h
+                    nc.tensor.transpose(
+                        xt[:, P * pos : P * pos + P], words[:, t, P * j : P * j + P], ident[:]
+                    )
+
+        def copy_x(c, t):
+            if t == 0:
+                st[c]["xg"] = xg_pool.tile([P, CMAX * FEAT], BF16, name="xg", align_bytes=64)
+            nc.vector.tensor_copy(
+                out=st[c]["xg"][:]
+                .bitcast(F32)[:, 512 * t : 512 * t + 512]
+                .rearrange("p (m u) -> p m u", u=2),
+                in_=st[c]["xt"][t][:].rearrange("p (u m) -> p m u", u=2),
+            )
+
+        def quantise(c, m, src):
+            n = CHUNKS[c]
+            nc.vector.quantize_mx(
+                out=st[c]["codes"][:, m, : 256 * n].bitcast(FP8X4),
+                scales=st[c]["scales"][:, m, : 256 * n],
+                in_=src[:, : FEAT * n],
+            )
+
+        def quantise_x(c):
+            st[c]["codes"] = cd_pool.tile([P, MAPS, CMAX * 256], U32, name="codes", align_bytes=64)
+            st[c]["scales"] = cd_pool.tile([P, MAPS, CMAX * 256], U8, name="scales", align_bytes=64)
+            quantise(c, 0, st[c]["xg"])
+
+        def split(c):
+            n = FEAT * CHUNKS[c]
+            na = n * ACT_SHARE_32 // 32
+            return n - na, na, n
+
+        def argument(c, g):
+            nd, na, n = split(c)
+            xg = st[c]["xg"]
+            ad = arg_pool.tile([P, CMAX * FEAT * (32 - ACT_SHARE_32) // 32], F32, name="ad")
+            aa = arg_pool.tile([P, CMAX * FEAT * ACT_SHARE_32 // 32], F32, name="aa")
+            st[c]["arg", g] = (ad, aa)
+            nc.vector.scalar_tensor_tensor(
+                out=ad[:, :nd],
+                in0=xg[:, :nd],
+                scalar=2.0 * CENTRES[g],
+                in1=xg[:, :nd],
+                op0=ALU.subtract,
+                op1=ALU.mult,
+            )
+            nc.scalar.activation(
+                out=aa[:, :na], in_=xg[:, nd:n], func=AF.Square, bias=shift[:, g : g + 1]
+            )
+
+        def exponential(c, g):
+            nd, na, n = split(c)
+            ad, aa = st[c]["arg", g]
+            rg = rg_pool.tile([P, CMAX * FEAT], BF16, name="rg", align_bytes=64)
+            st[c]["rg", g] = rg
+            nc.scalar.activation(
+                out=rg[:, :nd], in_=ad[:, :nd], func=AF.Exp, scale=-5.0, bias=shift[:, 8 + g : 9 + g]
+            )
+            nc.scalar.activation(out=rg[:, nd:n], in_=aa[:, :na], func=AF.Exp, scale=-5.0)
+
+        def quantise_rbf(c, g):
+            quantise(c, 1 + g, st[c]["rg", g])
+
+        def mx_group(c, t, acc, maps):
+            codes, scales = st[c]["codes"], st[c]["scales"]
+            steps = [(m, h) for m in maps for h in range(2)]
+            for i, (m, h) in enumerate(steps):
+                a = slice(P * (2 * t + h), P * (2 * t + h) + P)
+                b = slice(P * (2 * m + h), P * (2 * m + h) + P)
+                nc.tensor.matmul_mx(
+                    out=acc[:, P * t : P * t + P],
+                    lhsT=codes[:, m, a].bitcast(FP8X4),
+                    lhsT_scale=scales[:, m, a],
+                    rhs=w_codes[:, b].bitcast(FP8X4),
+                    rhs_scale=w_scales[:, b],
+                    start=(i == 0),
+                    stop=(i == len(steps) - 1),
+                )
+
+        def base_product(c):
+            st[c]["pb"] = acc_pool.tile([P, 512], F32, name="pb")
+            for t in range(CHUNKS[c]):
+                mx_group(c, t, st[c]["pb"], [0])
+
+        def spline_product(c):
+            st[c]["ps"] = acc_pool.tile([P, 512], F32, name="ps")
+            for t in range(CHUNKS[c]):
+                mx_group(c, t, st[c]["ps"], list(range(1, MAPS)))
+
+        def gate(c):
+            w = UNITS * CHUNKS[c]
+            st[c]["th"] = ep_pool.tile([P, 512], F32, name="th")
+            nc.scalar.activation(out=st[c]["th"][:, :w], in_=st[c]["pb"][:, :w], func=AF.Tanh, scale=0.5)
+
+        def silu_twice(c):
+            w = UNITS * CHUNKS[c]
+            st[c]["s2"] = ep_pool.tile([P, 512], F32, name="s2")
+            nc.vector.scalar_tensor_tensor(
+                out=st[c]["s2"][:, :w],
+                in0=st[c]["th"][:, :w],
+                scalar=1.0,
+                in1=st[c]["pb"][:, :w],
+                op0=ALU.add,
+                op1=ALU.mult,
+            )
+
+        def finish(c):
+            n = CHUNKS[c]
+            w = UNITS * n
+            res = ep_pool.tile([P, 512], F32, name="res")
+            nc.vector.scalar_tensor_tensor(
+                out=res[:, :w],
+                in0=st[c]["s2"][:, :w],
+                scalar=0.5,
+                in1=st[c]["ps"][:, :w],
+                op0=ALU.mult,
+                op1=ALU.add,
+            )
+            nc.sync.dma_start(
+                out=out[row0[c] : row0[c] + P * n, :].rearrange("(p t) u -> p (t u)", t=n),
+                in_=res[:, :w],
+            )
+
+        plan = []
+
+        def at(slot, phase, fn, *args):
+            plan.append((max(slot, 0), phase, fn, args))
+
+        at(0, 0, load, 0)
+        at(0, 0, load, 1)
+        at(0, 0, load_weights)
+        at(W_SLOT, 7, prepare_weights)
+        for c in range(n_chunks):
+            n0 = NG * c
+            at(n0 - 4, 1, transposes, c)
+            if c + 2 < n_chunks:
+                at(n0 - 4, 1, load, c + 2)
+            for t in range(CHUNKS[c]):
+                at(n0 - 3 if 2 * t < CHUNKS[c] else n0 - 2, 2, copy_x, c, t)
+            at(n0 - 1, 6, quantise_x, c)
+            for g in range(NG):
+                at(n0 + g, 3, argument, c, g)
+                at(n0 + g + 2, 4, exponential, c, g)
+                at(n0 + g + 3, 5, quantise_rbf, c, g)
+            b = max(n0 + 1, W_SLOT)
+            at(b, 8, base_product, c)
+            at(b + 1, 10, gate, c)
+            at(b + 2, 11, silu_twice, c)
+            at(max(n0 + NG + 2, W_SLOT), 9, spline_product, c)
+            at(max(n0 + NG + 3, b + 3), 12, finish, c)
+        for slot, phase, fn, args in sorted(plan, key=lambda e: (e[0], e[1])):
+            fn(*args)

@@ -18,10 +18,15 @@ NG = len(CENTRES)
 MAPS = 1 + NG
 FLOPS = 2 * ROWS * FEAT * UNITS * MAPS
 
-CHUNKS = (1, 1, 2) + (4,) * 10 + (2, 1, 1)
-CMAX = 4
-ACT_SHARE_32 = 7
-W_SLOT = 4
+CHUNKS = (1, 1) + (2,) * 22 + (1, 1)
+CMAX = 2
+ORDER = (2, 3, 1, 4, 0)
+POOL_SHARE_32 = (32, 16, 0, 0, 0)
+ACT_SHARE_32 = (0, 0, 0, 0, 14)
+FIRST_ACT_SHARE_32 = (32, 0, 0, 0, 0)
+W_ENGINE = "vector"
+LAG = 2
+W_PERIOD = 2
 
 
 def tile_kandense_t_kernel(tc, x, base_weight, spline_weight, out):
@@ -32,11 +37,11 @@ def tile_kandense_t_kernel(tc, x, base_weight, spline_weight, out):
 
     with ExitStack() as ctx:
         const = ctx.enter_context(tc.tile_pool(name="const", bufs=1))
-        xn_pool = ctx.enter_context(tc.tile_pool(name="xn", bufs=2))
+        xn_pool = ctx.enter_context(tc.tile_pool(name="xn", bufs=3))
         xg_pool = ctx.enter_context(tc.tile_pool(name="xg", bufs=2))
-        arg_pool = ctx.enter_context(tc.tile_pool(name="arg", bufs=3))
-        rg_pool = ctx.enter_context(tc.tile_pool(name="rg", bufs=3))
-        cd_pool = ctx.enter_context(tc.tile_pool(name="cd", bufs=2))
+        arg_pool = ctx.enter_context(tc.tile_pool(name="arg", bufs=7))
+        rg_pool = ctx.enter_context(tc.tile_pool(name="rg", bufs=10))
+        cd_pool = ctx.enter_context(tc.tile_pool(name="cd", bufs=3))
         ep_pool = ctx.enter_context(tc.tile_pool(name="ep", bufs=2))
         xt_pool = ctx.enter_context(tc.psum_pool(name="xt", bufs=4))
         acc_pool = ctx.enter_context(tc.psum_pool(name="acc", bufs=2))
@@ -79,56 +84,56 @@ def tile_kandense_t_kernel(tc, x, base_weight, spline_weight, out):
                 in_=spline_weight.rearrange("(a p e) c s -> p a (e c s)", a=4, p=P, e=2),
             )
 
-        def prepare_weights():
-            flat = w_grouped[:].rearrange("p m h c t -> p (m h c t)")
-            for h in range(2):
-                nc.vector.tensor_copy(
-                    out=w_grouped[:, 0, h].rearrange("p c (u e) -> p c u e", u=2),
-                    in_=wb_raw[:, 2 * h : 2 * h + 2, :].rearrange("p u (e c) -> p c u e", e=2),
-                )
-            nc.vector.quantize_mx(
-                out=w_codes[:, 0:256].bitcast(FP8X4), scales=w_scales[:, 0:256], in_=flat[:, 0:1024]
-            )
-            for g in range(NG):
+        def regroup_weights():
+            for m in range(MAPS):
                 for h in range(2):
-                    nc.vector.tensor_copy(
-                        out=w_grouped[:, 1 + g, h].rearrange("p c (u e) -> p c u e", u=2),
-                        in_=ws_raw[:, 2 * h : 2 * h + 2, :].rearrange(
+                    if m == 0:
+                        src = wb_raw[:, 2 * h : 2 * h + 2, :].rearrange("p u (e c) -> p c u e", e=2)
+                    else:
+                        src = ws_raw[:, 2 * h : 2 * h + 2, :].rearrange(
                             "p u (e c s) -> p c u e s", e=2, s=8
-                        )[:, :, :, :, g],
-                    )
-            nc.vector.quantize_mx(
-                out=w_codes[:, 256:1280].bitcast(FP8X4),
-                scales=w_scales[:, 256:1280],
-                in_=flat[:, 1024:5120],
-            )
-            nc.vector.quantize_mx(
-                out=w_codes[:, 1280:1536].bitcast(FP8X4),
-                scales=w_scales[:, 1280:1536],
-                in_=flat[:, 5120:6144],
-            )
+                        )[:, :, :, :, m - 1]
+                    if W_ENGINE == "gpsimd":
+                        nc.gpsimd.tensor_scalar(
+                            out=w_grouped[:, m, h].rearrange("p c (u e) -> p c u e", u=2),
+                            in0=src,
+                            scalar1=1.0,
+                            scalar2=0.0,
+                            op0=ALU.mult,
+                            op1=ALU.add,
+                        )
+                    else:
+                        nc.vector.tensor_copy(
+                            out=w_grouped[:, m, h].rearrange("p c (u e) -> p c u e", u=2), in_=src
+                        )
+
+        def quantise_weights():
+            flat = w_grouped[:].rearrange("p m h c t -> p (m h c t)")
+            for lo, hi in ((0, 1024), (1024, 1536)):
+                nc.vector.quantize_mx(
+                    out=w_codes[:, lo:hi].bitcast(FP8X4),
+                    scales=w_scales[:, lo:hi],
+                    in_=flat[:, 4 * lo : 4 * hi],
+                )
 
         def transposes(c):
             words = st[c]["xn"][:].bitcast(F32)
             st[c]["xt"] = []
             for t in range(CHUNKS[c]):
-                xt = xt_pool.tile([P, 512], F32, name="xt")
+                xt = xt_pool.tile([P, 256, 2], F32, name="xt")
                 st[c]["xt"].append(xt)
                 for j in range(4):
                     h, u = divmod(j, 2)
-                    pos = 2 * u + h
                     nc.tensor.transpose(
-                        xt[:, P * pos : P * pos + P], words[:, t, P * j : P * j + P], ident[:]
+                        xt[:, P * h : P * h + P, u], words[:, t, P * j : P * j + P], ident[:]
                     )
 
         def copy_x(c, t):
             if t == 0:
                 st[c]["xg"] = xg_pool.tile([P, CMAX * FEAT], BF16, name="xg", align_bytes=64)
             nc.vector.tensor_copy(
-                out=st[c]["xg"][:]
-                .bitcast(F32)[:, 512 * t : 512 * t + 512]
-                .rearrange("p (m u) -> p m u", u=2),
-                in_=st[c]["xt"][t][:].rearrange("p (u m) -> p m u", u=2),
+                out=st[c]["xg"][:].bitcast(F32)[:, 512 * t : 512 * t + 512],
+                in_=st[c]["xt"][t][:].rearrange("p m u -> p (m u)"),
             )
 
         def quantise(c, m, src):
@@ -144,41 +149,62 @@ def tile_kandense_t_kernel(tc, x, base_weight, spline_weight, out):
             st[c]["scales"] = cd_pool.tile([P, MAPS, CMAX * 256], U8, name="scales", align_bytes=64)
             quantise(c, 0, st[c]["xg"])
 
-        def split(c):
+        def split(c, pos):
             n = FEAT * CHUNKS[c]
-            na = n * ACT_SHARE_32 // 32
-            return n - na, na, n
+            if c == 0:
+                return 0, n - n * FIRST_ACT_SHARE_32[pos] // 32, n
+            return n * POOL_SHARE_32[pos] // 32, n - n * ACT_SHARE_32[pos] // 32, n
 
-        def argument(c, g):
-            nd, na, n = split(c)
+        def argument(c, pos):
+            g = ORDER[pos]
+            npl, nd, n = split(c, pos)
             xg = st[c]["xg"]
-            ad = arg_pool.tile([P, CMAX * FEAT * (32 - ACT_SHARE_32) // 32], F32, name="ad")
-            aa = arg_pool.tile([P, CMAX * FEAT * ACT_SHARE_32 // 32], F32, name="aa")
-            st[c]["arg", g] = (ad, aa)
-            nc.vector.scalar_tensor_tensor(
-                out=ad[:, :nd],
-                in0=xg[:, :nd],
-                scalar=2.0 * CENTRES[g],
-                in1=xg[:, :nd],
-                op0=ALU.subtract,
-                op1=ALU.mult,
-            )
-            nc.scalar.activation(
-                out=aa[:, :na], in_=xg[:, nd:n], func=AF.Square, bias=shift[:, g : g + 1]
-            )
+            arg = arg_pool.tile([P, CMAX * FEAT], F32, name="arg")
+            st[c]["arg", pos] = arg
+            if pos == 0 and npl > 0:
+                nc.gpsimd.tensor_tensor(
+                    out=arg[:, :npl], in0=xg[:, :npl], in1=xg[:, :npl], op=ALU.mult
+                )
+            elif npl > 0:
+                nc.gpsimd.tensor_tensor(
+                    out=arg[:, :npl], in0=st[c]["arg", 0][:, :npl], in1=xg[:, :npl], op=ALU.subtract
+                )
+            for t in range(CHUNKS[c]):
+                lo, hi = max(FEAT * t, npl), min(FEAT * t + FEAT, nd)
+                if hi > lo:
+                    bank = st[c]["xt"][t][:].rearrange("p m u -> p (m u)").bitcast(BF16)
+                    nc.vector.scalar_tensor_tensor(
+                        out=arg[:, lo:hi],
+                        in0=bank[:, lo - FEAT * t : hi - FEAT * t],
+                        scalar=2.0 * CENTRES[g],
+                        in1=xg[:, lo:hi],
+                        op0=ALU.subtract,
+                        op1=ALU.mult,
+                    )
+            if nd < n:
+                nc.scalar.activation(
+                    out=arg[:, nd:n], in_=xg[:, nd:n], func=AF.Square, bias=shift[:, g : g + 1]
+                )
 
-        def exponential(c, g):
-            nd, na, n = split(c)
-            ad, aa = st[c]["arg", g]
+        def exponential(c, pos):
+            g = ORDER[pos]
+            npl, nd, n = split(c, pos)
+            arg = st[c]["arg", pos]
             rg = rg_pool.tile([P, CMAX * FEAT], BF16, name="rg", align_bytes=64)
-            st[c]["rg", g] = rg
-            nc.scalar.activation(
-                out=rg[:, :nd], in_=ad[:, :nd], func=AF.Exp, scale=-5.0, bias=shift[:, 8 + g : 9 + g]
-            )
-            nc.scalar.activation(out=rg[:, nd:n], in_=aa[:, :na], func=AF.Exp, scale=-5.0)
+            st[c]["rg", pos] = rg
+            if nd > 0:
+                nc.scalar.activation(
+                    out=rg[:, :nd],
+                    in_=arg[:, :nd],
+                    func=AF.Exp,
+                    scale=-5.0,
+                    bias=shift[:, 8 + g : 9 + g],
+                )
+            if nd < n:
+                nc.scalar.activation(out=rg[:, nd:n], in_=arg[:, nd:n], func=AF.Exp, scale=-5.0)
 
-        def quantise_rbf(c, g):
-            quantise(c, 1 + g, st[c]["rg", g])
+        def quantise_rbf(c, pos):
+            quantise(c, 1 + ORDER[pos], st[c]["rg", pos])
 
         def mx_group(c, t, acc, maps):
             codes, scales = st[c]["codes"], st[c]["scales"]
@@ -196,24 +222,18 @@ def tile_kandense_t_kernel(tc, x, base_weight, spline_weight, out):
                     stop=(i == len(steps) - 1),
                 )
 
-        def base_product(c):
-            st[c]["pb"] = acc_pool.tile([P, 512], F32, name="pb")
-            for t in range(CHUNKS[c]):
-                mx_group(c, t, st[c]["pb"], [0])
-
-        def spline_product(c):
-            st[c]["ps"] = acc_pool.tile([P, 512], F32, name="ps")
-            for t in range(CHUNKS[c]):
-                mx_group(c, t, st[c]["ps"], list(range(1, MAPS)))
-
-        def gate(c):
+        def base_part(c):
             w = UNITS * CHUNKS[c]
-            st[c]["th"] = ep_pool.tile([P, 512], F32, name="th")
-            nc.scalar.activation(out=st[c]["th"][:, :w], in_=st[c]["pb"][:, :w], func=AF.Tanh, scale=0.5)
+            pb = acc_pool.tile([P, 512], F32, name="pb")
+            for t in range(CHUNKS[c]):
+                mx_group(c, t, pb, [0])
+            th = ep_pool.tile([P, UNITS * CMAX], F32, name="th")
+            nc.scalar.activation(out=th[:, :w], in_=pb[:, :w], func=AF.Tanh, scale=0.5)
+            st[c]["th"], st[c]["pb"] = th, pb
 
         def silu_twice(c):
             w = UNITS * CHUNKS[c]
-            st[c]["s2"] = ep_pool.tile([P, 512], F32, name="s2")
+            st[c]["s2"] = ep_pool.tile([P, UNITS * CMAX], F32, name="s2", bufs=4)
             nc.vector.scalar_tensor_tensor(
                 out=st[c]["s2"][:, :w],
                 in0=st[c]["th"][:, :w],
@@ -223,10 +243,15 @@ def tile_kandense_t_kernel(tc, x, base_weight, spline_weight, out):
                 op1=ALU.mult,
             )
 
+        def spline_product(c):
+            st[c]["ps"] = acc_pool.tile([P, 512], F32, name="ps")
+            for t in range(CHUNKS[c]):
+                mx_group(c, t, st[c]["ps"], list(range(1, MAPS)))
+
         def finish(c):
             n = CHUNKS[c]
             w = UNITS * n
-            res = ep_pool.tile([P, 512], F32, name="res")
+            res = ep_pool.tile([P, UNITS * CMAX], F32, name="res")
             nc.vector.scalar_tensor_tensor(
                 out=res[:, :w],
                 in0=st[c]["s2"][:, :w],
@@ -240,32 +265,54 @@ def tile_kandense_t_kernel(tc, x, base_weight, spline_weight, out):
                 in_=res[:, :w],
             )
 
-        plan = []
+        def live(c):
+            return 0 <= c < n_chunks
 
-        def at(slot, phase, fn, *args):
-            plan.append((max(slot, 0), phase, fn, args))
+        load(0)
+        load(1)
+        load_weights()
+        load(2)
+        transposes(0)
+        transposes(1)
+        load(3)
+        done = [0]
 
-        at(0, 0, load, 0)
-        at(0, 0, load, 1)
-        at(0, 0, load_weights)
-        at(W_SLOT, 7, prepare_weights)
-        for c in range(n_chunks):
-            n0 = NG * c
-            at(n0 - 4, 1, transposes, c)
-            if c + 2 < n_chunks:
-                at(n0 - 4, 1, load, c + 2)
-            for t in range(CHUNKS[c]):
-                at(n0 - 3 if 2 * t < CHUNKS[c] else n0 - 2, 2, copy_x, c, t)
-            at(n0 - 1, 6, quantise_x, c)
-            for g in range(NG):
-                at(n0 + g, 3, argument, c, g)
-                at(n0 + g + 2, 4, exponential, c, g)
-                at(n0 + g + 3, 5, quantise_rbf, c, g)
-            b = max(n0 + 1, W_SLOT)
-            at(b, 8, base_product, c)
-            at(b + 1, 10, gate, c)
-            at(b + 2, 11, silu_twice, c)
-            at(max(n0 + NG + 2, W_SLOT), 9, spline_product, c)
-            at(max(n0 + NG + 3, b + 3), 12, finish, c)
-        for slot, phase, fn, args in sorted(plan, key=lambda e: (e[0], e[1])):
-            fn(*args)
+        def quantise_up_to(unit):
+            while done[0] < min(unit, NG * n_chunks):
+                quantise_rbf(done[0] // NG, done[0] % NG)
+                done[0] += 1
+
+        for k in range(-1, n_chunks + 2):
+            if k >= 0 and live(k + 2):
+                transposes(k + 2)
+            if k >= 0 and live(k + 4):
+                load(k + 4)
+            if live(k):
+                quantise_x(k)
+            quantise_up_to(NG * k - LAG)
+            if k == W_PERIOD:
+                quantise_weights()
+            if live(k - 2):
+                spline_product(k - 2)
+            if live(k + 1):
+                for t in range(CHUNKS[k + 1]):
+                    copy_x(k + 1, t)
+            for pos in range(NG):
+                if live(k + 1):
+                    argument(k + 1, pos)
+                if live(k):
+                    exponential(k, pos)
+                    if not live(k + 1):
+                        quantise_up_to(NG * k + pos)
+                if pos == 2 and live(k) and k > W_PERIOD:
+                    base_part(k)
+            if k == W_PERIOD - 1:
+                regroup_weights()
+            if k == W_PERIOD:
+                for c in range(W_PERIOD + 1):
+                    base_part(c)
+                    silu_twice(c)
+            if live(k - 2):
+                finish(k - 2)
+            if live(k) and k > W_PERIOD:
+                silu_twice(k)

@@ -21,9 +21,10 @@ FLOPS = 2 * ROWS * FEAT * UNITS * MAPS
 CHUNKS = (1, 1) + (2,) * 22 + (1, 1)
 CMAX = 2
 ORDER = (2, 3, 1, 4, 0)
-POOL_SHARE_32 = (32, 16, 0, 0, 0)
-ACT_SHARE_32 = (0, 0, 0, 0, 14)
-FIRST_ACT_SHARE_32 = (32, 0, 0, 0, 0)
+POOL_SHARE_32 = (32, 16, 8, 0, 0)
+ACT_SHARE_32 = (0, 0, 0, 0, 10)
+ACT_SHARE_OF_CHUNK = {0: (32, 0, 0, 0, 0), 3: (0, 0, 0, 16, 32)}
+XC_EARLY = True
 W_ENGINE = "vector"
 LAG = 2
 W_PERIOD = 2
@@ -151,9 +152,8 @@ def tile_kandense_t_kernel(tc, x, base_weight, spline_weight, out):
 
         def split(c, pos):
             n = FEAT * CHUNKS[c]
-            if c == 0:
-                return 0, n - n * FIRST_ACT_SHARE_32[pos] // 32, n
-            return n * POOL_SHARE_32[pos] // 32, n - n * ACT_SHARE_32[pos] // 32, n
+            share = ACT_SHARE_OF_CHUNK.get(c, ACT_SHARE_32)[pos]
+            return (0 if c == 0 else n * POOL_SHARE_32[pos] // 32), n - n * share // 32, n
 
         def argument(c, pos):
             g = ORDER[pos]
@@ -167,7 +167,10 @@ def tile_kandense_t_kernel(tc, x, base_weight, spline_weight, out):
                 )
             elif npl > 0:
                 nc.gpsimd.tensor_tensor(
-                    out=arg[:, :npl], in0=st[c]["arg", 0][:, :npl], in1=xg[:, :npl], op=ALU.subtract
+                    out=arg[:, :npl],
+                    in0=st[c]["arg", 0][:, :npl],
+                    in1=xg[:, :npl],
+                    op=(ALU.subtract if CENTRES[g] > 0 else ALU.add),
                 )
             for t in range(CHUNKS[c]):
                 lo, hi = max(FEAT * t, npl), min(FEAT * t + FEAT, nd)
@@ -246,7 +249,7 @@ def tile_kandense_t_kernel(tc, x, base_weight, spline_weight, out):
         def spline_product(c):
             st[c]["ps"] = acc_pool.tile([P, 512], F32, name="ps")
             for t in range(CHUNKS[c]):
-                mx_group(c, t, st[c]["ps"], list(range(1, MAPS)))
+                mx_group(c, t, st[c]["ps"], [1 + g for g in ORDER])
 
         def finish(c):
             n = CHUNKS[c]
@@ -287,14 +290,18 @@ def tile_kandense_t_kernel(tc, x, base_weight, spline_weight, out):
                 transposes(k + 2)
             if k >= 0 and live(k + 4):
                 load(k + 4)
+            if XC_EARLY and live(k + 1):
+                for t in range(CHUNKS[k + 1]):
+                    copy_x(k + 1, t)
             if live(k):
                 quantise_x(k)
             quantise_up_to(NG * k - LAG)
             if k == W_PERIOD:
+                regroup_weights()
                 quantise_weights()
             if live(k - 2):
                 spline_product(k - 2)
-            if live(k + 1):
+            if not XC_EARLY and live(k + 1):
                 for t in range(CHUNKS[k + 1]):
                     copy_x(k + 1, t)
             for pos in range(NG):
@@ -306,8 +313,6 @@ def tile_kandense_t_kernel(tc, x, base_weight, spline_weight, out):
                         quantise_up_to(NG * k + pos)
                 if pos == 2 and live(k) and k > W_PERIOD:
                     base_part(k)
-            if k == W_PERIOD - 1:
-                regroup_weights()
             if k == W_PERIOD:
                 for c in range(W_PERIOD + 1):
                     base_part(c)

@@ -21,8 +21,8 @@ FLOPS = 2 * ROWS * FEAT * UNITS * MAPS
 CHUNKS = (1, 1) + (2,) * 22 + (1, 1)
 CMAX = 2
 ORDER = (2, 3, 1, 4, 0)
-POOL_SHARE_32 = (32, 16, 8, 0, 0)
-ACT_SHARE_32 = (0, 0, 0, 0, 10)
+POOL_SHARE_32 = (32, 16, 10, 0, 0)
+ACT_SHARE_32 = (0, 0, 0, 0, 11)
 ACT_SHARE_OF_CHUNK = {0: (32, 0, 0, 0, 0), 3: (0, 0, 0, 16, 32)}
 XC_EARLY = True
 W_ENGINE = "vector"

@@ -21,7 +21,7 @@ FLOPS = 2 * ROWS * FEAT * UNITS * MAPS
 CHUNKS = (1, 1) + (2,) * 22 + (1, 1)
 CMAX = 2
 ORDER = (2, 3, 1, 4, 0)
-POOL_SHARE_32 = (32, 16, 10, 0, 0)
+POOL_SHARE_32 = (32, 16, 6, 0, 0)
 ACT_SHARE_32 = (0, 0, 0, 0, 11)
 ACT_SHARE_OF_CHUNK = {0: (32, 0, 0, 0, 0), 3: (0, 0, 0, 16, 32)}
 XC_EARLY = True

@@ -21,8 +21,8 @@ FLOPS = 2 * ROWS * FEAT * UNITS * MAPS
 CHUNKS = (1, 1) + (2,) * 22 + (1, 1)
 CMAX = 2
 ORDER = (2, 3, 1, 4, 0)
-POOL_SHARE_32 = (32, 16, 6, 0, 0)
-ACT_SHARE_32 = (0, 0, 0, 0, 11)
+POOL_SHARE_32 = (32, 24, 0, 0, 0)
+ACT_SHARE_32 = (0, 0, 0, 0, 10)
 ACT_SHARE_OF_CHUNK = {0: (32, 0, 0, 0, 0), 3: (0, 0, 0, 16, 32)}
 XC_EARLY = True
 W_ENGINE = "vector"

@@ -20,13 +20,9 @@ FLOPS = 2 * ROWS * FEAT * UNITS * MAPS
 
 CHUNKS = (1, 1) + (2,) * 22 + (1, 1)
 CMAX = 2
-ORDER = (2, 3, 1, 4, 0)
-POOL_SHARE_32 = (32, 24, 0, 0, 0)
-ACT_SHARE_32 = (0, 0, 0, 0, 10)
-ACT_SHARE_OF_CHUNK = {0: (32, 0, 0, 0, 0), 3: (0, 0, 0, 16, 32)}
-XC_EARLY = True
-W_ENGINE = "vector"
-LAG = 2
+ORDER = (1, 3, 0, 4, 2)
+ON_VECTOR = (1, 0)
+LAG = 1
 W_PERIOD = 2
 
 
@@ -38,22 +34,28 @@ def tile_kandense_t_kernel(tc, x, base_weight, spline_weight, out):
 
     with ExitStack() as ctx:
         const = ctx.enter_context(tc.tile_pool(name="const", bufs=1))
-        xn_pool = ctx.enter_context(tc.tile_pool(name="xn", bufs=3))
-        xg_pool = ctx.enter_context(tc.tile_pool(name="xg", bufs=2))
-        arg_pool = ctx.enter_context(tc.tile_pool(name="arg", bufs=7))
-        rg_pool = ctx.enter_context(tc.tile_pool(name="rg", bufs=10))
+        tok_pool = ctx.enter_context(tc.tile_pool(name="tok", bufs=3))
+        xn_pool = ctx.enter_context(tc.tile_pool(name="xn", bufs=4))
+        nat_pool = ctx.enter_context(tc.tile_pool(name="nat", bufs=3))
+        xg_pool = ctx.enter_context(tc.tile_pool(name="xg", bufs=3))
+        arg_pool = ctx.enter_context(tc.tile_pool(name="arg", bufs=4))
+        rg_pool = ctx.enter_context(tc.tile_pool(name="rg", bufs=8))
         cd_pool = ctx.enter_context(tc.tile_pool(name="cd", bufs=3))
         ep_pool = ctx.enter_context(tc.tile_pool(name="ep", bufs=2))
-        xt_pool = ctx.enter_context(tc.psum_pool(name="xt", bufs=4))
+        xt_pool = ctx.enter_context(tc.psum_pool(name="xt", bufs=2))
+        ab_pool = ctx.enter_context(tc.psum_pool(name="ab", bufs=4))
         acc_pool = ctx.enter_context(tc.psum_pool(name="acc", bufs=2))
         ctx.enter_context(tc.manual_schedule())
 
         ident = const.tile([P, P], F32, name="ident")
         make_identity(nc, ident[:])
-        shift = const.tile([P, 2 * 8], F32, name="shift")
+        minus_two = const.tile([P, P], BF16, name="minus_two")
+        nc.vector.tensor_scalar(
+            out=minus_two[:], in0=ident[:], scalar1=-2.0, scalar2=None, op0=ALU.mult
+        )
+        shift = const.tile([P, 8], F32, name="shift")
         for g in range(NG):
-            nc.vector.memset(shift[:, g : g + 1], -CENTRES[g])
-            nc.vector.memset(shift[:, 8 + g : 9 + g], -5.0 * CENTRES[g] * CENTRES[g])
+            nc.vector.memset(shift[:, g : g + 1], -5.0 * CENTRES[g] * CENTRES[g])
         warm_in = const.tile([P, 1], F32, name="warm_in")
         warm_out = const.tile([P, 1], F32, name="warm_out")
         nc.vector.memset(warm_in[:], 0.0)
@@ -66,6 +68,7 @@ def tile_kandense_t_kernel(tc, x, base_weight, spline_weight, out):
         w_scales = const.tile([P, MAPS * 2 * UNITS], U8, name="w_scales", align_bytes=64)
 
         st = [dict() for c in range(n_chunks)]
+        token = [None]
 
         def load(c):
             n = CHUNKS[c]
@@ -94,19 +97,9 @@ def tile_kandense_t_kernel(tc, x, base_weight, spline_weight, out):
                         src = ws_raw[:, 2 * h : 2 * h + 2, :].rearrange(
                             "p u (e c s) -> p c u e s", e=2, s=8
                         )[:, :, :, :, m - 1]
-                    if W_ENGINE == "gpsimd":
-                        nc.gpsimd.tensor_scalar(
-                            out=w_grouped[:, m, h].rearrange("p c (u e) -> p c u e", u=2),
-                            in0=src,
-                            scalar1=1.0,
-                            scalar2=0.0,
-                            op0=ALU.mult,
-                            op1=ALU.add,
-                        )
-                    else:
-                        nc.vector.tensor_copy(
-                            out=w_grouped[:, m, h].rearrange("p c (u e) -> p c u e", u=2), in_=src
-                        )
+                    nc.vector.tensor_copy(
+                        out=w_grouped[:, m, h].rearrange("p c (u e) -> p c u e", u=2), in_=src
+                    )
 
         def quantise_weights():
             flat = w_grouped[:].rearrange("p m h c t -> p (m h c t)")
@@ -116,6 +109,31 @@ def tile_kandense_t_kernel(tc, x, base_weight, spline_weight, out):
                     scales=w_scales[:, lo:hi],
                     in_=flat[:, 4 * lo : 4 * hi],
                 )
+
+        def new_token():
+            token[0] = tok_pool.tile([P, 1], F32, name="tok")
+            nc.vector.memset(token[0][:], -1.0)
+
+        def natural(c):
+            n = CHUNKS[c]
+            src = st[c]["xn"][:, :n, :].rearrange("q t (j p e) -> q (t j) e p", j=4, e=2)
+            neg = nat_pool.tile([P, CMAX * 8, P], F32, name="neg")
+            sq = nat_pool.tile([P, CMAX * 8, P], F32, name="sq")
+            nc.gpsimd.tensor_scalar(
+                out=neg[:, : 8 * n, :].rearrange("q (a e) p -> q a e p", e=2),
+                in0=src,
+                scalar1=token[0][:],
+                scalar2=0.0,
+                op0=ALU.mult,
+                op1=ALU.add,
+            )
+            nc.gpsimd.tensor_tensor(
+                out=sq[:, : 8 * n, :].rearrange("q (a e) p -> q a e p", e=2),
+                in0=src,
+                in1=src,
+                op=ALU.mult,
+            )
+            st[c]["neg"], st[c]["sq"] = neg, sq
 
         def transposes(c):
             words = st[c]["xn"][:].bitcast(F32)
@@ -129,13 +147,13 @@ def tile_kandense_t_kernel(tc, x, base_weight, spline_weight, out):
                         xt[:, P * h : P * h + P, u], words[:, t, P * j : P * j + P], ident[:]
                     )
 
-        def copy_x(c, t):
-            if t == 0:
-                st[c]["xg"] = xg_pool.tile([P, CMAX * FEAT], BF16, name="xg", align_bytes=64)
-            nc.vector.tensor_copy(
-                out=st[c]["xg"][:].bitcast(F32)[:, 512 * t : 512 * t + 512],
-                in_=st[c]["xt"][t][:].rearrange("p m u -> p (m u)"),
-            )
+        def copy_x(c):
+            st[c]["xg"] = xg_pool.tile([P, CMAX * FEAT], BF16, name="xg", align_bytes=64)
+            for t in range(CHUNKS[c]):
+                nc.vector.tensor_copy(
+                    out=st[c]["xg"][:].bitcast(F32)[:, 512 * t : 512 * t + 512],
+                    in_=st[c]["xt"][t][:].rearrange("p m u -> p (m u)"),
+                )
 
         def quantise(c, m, src):
             n = CHUNKS[c]
@@ -150,73 +168,82 @@ def tile_kandense_t_kernel(tc, x, base_weight, spline_weight, out):
             st[c]["scales"] = cd_pool.tile([P, MAPS, CMAX * 256], U8, name="scales", align_bytes=64)
             quantise(c, 0, st[c]["xg"])
 
-        def split(c, pos):
-            n = FEAT * CHUNKS[c]
-            share = ACT_SHARE_OF_CHUNK.get(c, ACT_SHARE_32)[pos]
-            return (0 if c == 0 else n * POOL_SHARE_32[pos] // 32), n - n * share // 32, n
-
-        def argument(c, pos):
-            g = ORDER[pos]
-            npl, nd, n = split(c, pos)
-            xg = st[c]["xg"]
+        def vector_argument(c, g):
             arg = arg_pool.tile([P, CMAX * FEAT], F32, name="arg")
-            st[c]["arg", pos] = arg
-            if pos == 0 and npl > 0:
-                nc.gpsimd.tensor_tensor(
-                    out=arg[:, :npl], in0=xg[:, :npl], in1=xg[:, :npl], op=ALU.mult
-                )
-            elif npl > 0:
-                nc.gpsimd.tensor_tensor(
-                    out=arg[:, :npl],
-                    in0=st[c]["arg", 0][:, :npl],
-                    in1=xg[:, :npl],
-                    op=(ALU.subtract if CENTRES[g] > 0 else ALU.add),
-                )
+            st[c]["arg", g] = arg
             for t in range(CHUNKS[c]):
-                lo, hi = max(FEAT * t, npl), min(FEAT * t + FEAT, nd)
-                if hi > lo:
-                    bank = st[c]["xt"][t][:].rearrange("p m u -> p (m u)").bitcast(BF16)
-                    nc.vector.scalar_tensor_tensor(
-                        out=arg[:, lo:hi],
-                        in0=bank[:, lo - FEAT * t : hi - FEAT * t],
-                        scalar=2.0 * CENTRES[g],
-                        in1=xg[:, lo:hi],
-                        op0=ALU.subtract,
-                        op1=ALU.mult,
-                    )
-            if nd < n:
-                nc.scalar.activation(
-                    out=arg[:, nd:n], in_=xg[:, nd:n], func=AF.Square, bias=shift[:, g : g + 1]
+                nc.vector.scalar_tensor_tensor(
+                    out=arg[:, FEAT * t : FEAT * t + FEAT],
+                    in0=st[c]["xt"][t][:].rearrange("p m u -> p (m u)").bitcast(BF16),
+                    scalar=2.0 * CENTRES[g],
+                    in1=st[c]["xg"][:, FEAT * t : FEAT * t + FEAT],
+                    op0=ALU.subtract,
+                    op1=ALU.mult,
                 )
+
+        def tensor_argument(c, g):
+            banks = []
+            for t in range(CHUNKS[c]):
+                for h in range(2):
+                    bank = ab_pool.tile([P, 4, P], F32, name="bank")
+                    banks.append(bank)
+                    for s in range(4):
+                        b = 8 * t + 4 * h + s
+                        sq, neg = st[c]["sq"][:, b, :], st[c]["neg"][:, b, :]
+                        terms = [sq]
+                        plain = g == 4 and t == 0
+                        if not plain:
+                            terms = terms + [neg] * (g - 2)
+                        for i, term in enumerate(terms):
+                            nc.tensor.matmul(
+                                bank[:, s, :],
+                                term,
+                                ident[:],
+                                start=(i == 0),
+                                stop=(i == len(terms) - 1 and not plain),
+                                is_transpose=True,
+                            )
+                        if plain:
+                            base = FEAT * t + 512 * h
+                            nc.tensor.matmul(
+                                bank[:, s, :],
+                                minus_two[:],
+                                st[c]["xg"][:, base : base + 512].rearrange(
+                                    "p (m s) -> p m s", s=4
+                                )[:, :, s],
+                                start=False,
+                                stop=True,
+                            )
+            st[c]["arg", g] = banks
 
         def exponential(c, pos):
             g = ORDER[pos]
-            npl, nd, n = split(c, pos)
-            arg = st[c]["arg", pos]
+            n = FEAT * CHUNKS[c]
             rg = rg_pool.tile([P, CMAX * FEAT], BF16, name="rg", align_bytes=64)
             st[c]["rg", pos] = rg
-            if nd > 0:
+            bias = shift[:, g : g + 1]
+            if g in ON_VECTOR:
                 nc.scalar.activation(
-                    out=rg[:, :nd],
-                    in_=arg[:, :nd],
-                    func=AF.Exp,
-                    scale=-5.0,
-                    bias=shift[:, 8 + g : 9 + g],
+                    out=rg[:, :n], in_=st[c]["arg", g][:, :n], func=AF.Exp, scale=-5.0, bias=bias
                 )
-            if nd < n:
-                nc.scalar.activation(out=rg[:, nd:n], in_=arg[:, nd:n], func=AF.Exp, scale=-5.0)
+            else:
+                for q, bank in enumerate(st[c]["arg", g]):
+                    nc.scalar.activation(
+                        out=rg[:, 512 * q : 512 * q + 512].rearrange("p (m s) -> p m s", s=4),
+                        in_=bank[:].rearrange("p s m -> p m s"),
+                        func=AF.Exp,
+                        scale=-5.0,
+                        bias=bias,
+                    )
 
-        def quantise_rbf(c, pos):
-            quantise(c, 1 + ORDER[pos], st[c]["rg", pos])
-
-        def mx_group(c, t, acc, maps):
-            codes, scales = st[c]["codes"], st[c]["scales"]
+        def mx_group(c, t, lo, maps):
+            codes, scales, acc = st[c]["codes"], st[c]["scales"], st[c]["acc"]
             steps = [(m, h) for m in maps for h in range(2)]
             for i, (m, h) in enumerate(steps):
                 a = slice(P * (2 * t + h), P * (2 * t + h) + P)
                 b = slice(P * (2 * m + h), P * (2 * m + h) + P)
                 nc.tensor.matmul_mx(
-                    out=acc[:, P * t : P * t + P],
+                    out=acc[:, lo + P * t : lo + P * t + P],
                     lhsT=codes[:, m, a].bitcast(FP8X4),
                     lhsT_scale=scales[:, m, a],
                     rhs=w_codes[:, b].bitcast(FP8X4),
@@ -225,41 +252,39 @@ def tile_kandense_t_kernel(tc, x, base_weight, spline_weight, out):
                     stop=(i == len(steps) - 1),
                 )
 
-        def base_part(c):
-            w = UNITS * CHUNKS[c]
-            pb = acc_pool.tile([P, 512], F32, name="pb")
+        def products(c):
+            st[c]["acc"] = acc_pool.tile([P, 512], F32, name="acc")
             for t in range(CHUNKS[c]):
-                mx_group(c, t, pb, [0])
-            th = ep_pool.tile([P, UNITS * CMAX], F32, name="th")
-            nc.scalar.activation(out=th[:, :w], in_=pb[:, :w], func=AF.Tanh, scale=0.5)
-            st[c]["th"], st[c]["pb"] = th, pb
+                mx_group(c, t, 0, [0])
+            for t in range(CHUNKS[c]):
+                mx_group(c, t, 256, [1 + g for g in ORDER])
 
-        def silu_twice(c):
+        def half_tanh(c):
             w = UNITS * CHUNKS[c]
-            st[c]["s2"] = ep_pool.tile([P, UNITS * CMAX], F32, name="s2", bufs=4)
-            nc.vector.scalar_tensor_tensor(
-                out=st[c]["s2"][:, :w],
-                in0=st[c]["th"][:, :w],
-                scalar=1.0,
-                in1=st[c]["pb"][:, :w],
-                op0=ALU.add,
-                op1=ALU.mult,
+            st[c]["th"] = ep_pool.tile([P, UNITS * CMAX], F32, name="th")
+            nc.scalar.activation(
+                out=st[c]["th"][:, :w], in_=st[c]["acc"][:, :w], func=AF.Tanh, scale=0.5
             )
-
-        def spline_product(c):
-            st[c]["ps"] = acc_pool.tile([P, 512], F32, name="ps")
-            for t in range(CHUNKS[c]):
-                mx_group(c, t, st[c]["ps"], [1 + g for g in ORDER])
 
         def finish(c):
             n = CHUNKS[c]
             w = UNITS * n
+            acc = st[c]["acc"]
+            s2 = ep_pool.tile([P, UNITS * CMAX], F32, name="s2")
+            nc.vector.scalar_tensor_tensor(
+                out=s2[:, :w],
+                in0=st[c]["th"][:, :w],
+                scalar=1.0,
+                in1=acc[:, :w],
+                op0=ALU.add,
+                op1=ALU.mult,
+            )
             res = ep_pool.tile([P, UNITS * CMAX], F32, name="res")
             nc.vector.scalar_tensor_tensor(
                 out=res[:, :w],
-                in0=st[c]["s2"][:, :w],
+                in0=s2[:, :w],
                 scalar=0.5,
-                in1=st[c]["ps"][:, :w],
+                in1=acc[:, 256 : 256 + w],
                 op0=ALU.mult,
                 op1=ALU.add,
             )
@@ -271,53 +296,62 @@ def tile_kandense_t_kernel(tc, x, base_weight, spline_weight, out):
         def live(c):
             return 0 <= c < n_chunks
 
-        load(0)
-        load(1)
-        load_weights()
-        load(2)
-        transposes(0)
-        transposes(1)
-        load(3)
         done = [0]
 
         def quantise_up_to(unit):
             while done[0] < min(unit, NG * n_chunks):
-                quantise_rbf(done[0] // NG, done[0] % NG)
+                c, pos = divmod(done[0], NG)
+                quantise(c, 1 + ORDER[pos], st[c]["rg", pos])
                 done[0] += 1
 
-        for k in range(-1, n_chunks + 2):
-            if k >= 0 and live(k + 2):
-                transposes(k + 2)
-            if k >= 0 and live(k + 4):
+        load(0)
+        load(1)
+        load_weights()
+        load(2)
+        load(3)
+        new_token()
+        natural(0)
+        transposes(0)
+        copy_x(0)
+        for g in ON_VECTOR:
+            vector_argument(0, g)
+        natural(1)
+
+        for k in range(n_chunks + 2):
+            if live(k):
+                tensor_argument(k, ORDER[1])
+            if live(k + 1):
+                transposes(k + 1)
+            if live(k + 4):
                 load(k + 4)
-            if XC_EARLY and live(k + 1):
-                for t in range(CHUNKS[k + 1]):
-                    copy_x(k + 1, t)
+            quantise_up_to(NG * k - LAG if live(k) else NG * n_chunks)
             if live(k):
                 quantise_x(k)
-            quantise_up_to(NG * k - LAG)
             if k == W_PERIOD:
                 regroup_weights()
                 quantise_weights()
-            if live(k - 2):
-                spline_product(k - 2)
-            if not XC_EARLY and live(k + 1):
-                for t in range(CHUNKS[k + 1]):
-                    copy_x(k + 1, t)
-            for pos in range(NG):
-                if live(k + 1):
-                    argument(k + 1, pos)
-                if live(k):
-                    exponential(k, pos)
-                    if not live(k + 1):
-                        quantise_up_to(NG * k + pos)
-                if pos == 2 and live(k) and k > W_PERIOD:
-                    base_part(k)
+            new_token()
+            if live(k + 2):
+                natural(k + 2)
+            if live(k + 1):
+                copy_x(k + 1)
+            if live(k):
+                exponential(k, 0)
+                exponential(k, 1)
+            if live(k - 2) and k != W_PERIOD:
+                products(k - 2)
+                half_tanh(k - 2)
+            if live(k):
+                tensor_argument(k, ORDER[3])
+                exponential(k, 2)
+                exponential(k, 3)
+                tensor_argument(k, ORDER[4])
+                exponential(k, 4)
             if k == W_PERIOD:
-                for c in range(W_PERIOD + 1):
-                    base_part(c)
-                    silu_twice(c)
+                products(k - 2)
+                half_tanh(k - 2)
+            if live(k + 1):
+                for g in ON_VECTOR:
+                    vector_argument(k + 1, g)
             if live(k - 2):
                 finish(k - 2)
-            if live(k) and k > W_PERIOD:
-                silu_twice(k)

@@ -38,7 +38,7 @@ def tile_kandense_t_kernel(tc, x, base_weight, spline_weight, out):
         xn_pool = ctx.enter_context(tc.tile_pool(name="xn", bufs=4))
         nat_pool = ctx.enter_context(tc.tile_pool(name="nat", bufs=3))
         xg_pool = ctx.enter_context(tc.tile_pool(name="xg", bufs=3))
-        arg_pool = ctx.enter_context(tc.tile_pool(name="arg", bufs=4))
+        arg_pool = ctx.enter_context(tc.tile_pool(name="arg", bufs=5))
         rg_pool = ctx.enter_context(tc.tile_pool(name="rg", bufs=8))
         cd_pool = ctx.enter_context(tc.tile_pool(name="cd", bufs=3))
         ep_pool = ctx.enter_context(tc.tile_pool(name="ep", bufs=2))
@@ -168,10 +168,10 @@ def tile_kandense_t_kernel(tc, x, base_weight, spline_weight, out):
             st[c]["scales"] = cd_pool.tile([P, MAPS, CMAX * 256], U8, name="scales", align_bytes=64)
             quantise(c, 0, st[c]["xg"])
 
-        def vector_argument(c, g):
+        def vector_argument(c, g, first=0):
             arg = arg_pool.tile([P, CMAX * FEAT], F32, name="arg")
-            st[c]["arg", g] = arg
-            for t in range(CHUNKS[c]):
+            st[c]["arg", g, "sbuf"] = arg
+            for t in range(first, CHUNKS[c]):
                 nc.vector.scalar_tensor_tensor(
                     out=arg[:, FEAT * t : FEAT * t + FEAT],
                     in0=st[c]["xt"][t][:].rearrange("p m u -> p (m u)").bitcast(BF16),
@@ -184,6 +184,8 @@ def tile_kandense_t_kernel(tc, x, base_weight, spline_weight, out):
         def tensor_argument(c, g):
             banks = []
             for t in range(CHUNKS[c]):
+                if g == 4 and t == 1:
+                    break
                 for h in range(2):
                     bank = ab_pool.tile([P, 4, P], F32, name="bank")
                     banks.append(bank)
@@ -224,13 +226,25 @@ def tile_kandense_t_kernel(tc, x, base_weight, spline_weight, out):
             bias = shift[:, g : g + 1]
             if g in ON_VECTOR:
                 nc.scalar.activation(
-                    out=rg[:, :n], in_=st[c]["arg", g][:, :n], func=AF.Exp, scale=-5.0, bias=bias
+                    out=rg[:, :n],
+                    in_=st[c]["arg", g, "sbuf"][:, :n],
+                    func=AF.Exp,
+                    scale=-5.0,
+                    bias=bias,
                 )
             else:
                 for q, bank in enumerate(st[c]["arg", g]):
                     nc.scalar.activation(
                         out=rg[:, 512 * q : 512 * q + 512].rearrange("p (m s) -> p m s", s=4),
                         in_=bank[:].rearrange("p s m -> p m s"),
+                        func=AF.Exp,
+                        scale=-5.0,
+                        bias=bias,
+                    )
+                if g == 4 and n > FEAT:
+                    nc.scalar.activation(
+                        out=rg[:, FEAT:n],
+                        in_=st[c]["arg", g, "sbuf"][:, FEAT:n],
                         func=AF.Exp,
                         scale=-5.0,
                         bias=bias,
@@ -353,5 +367,7 @@ def tile_kandense_t_kernel(tc, x, base_weight, spline_weight, out):
             if live(k + 1):
                 for g in ON_VECTOR:
                     vector_argument(k + 1, g)
+                if CHUNKS[k + 1] > 1:
+                    vector_argument(k + 1, 4, 1)
             if live(k - 2):
                 finish(k - 2)

@@ -49,9 +49,9 @@ def tile_kandense_t_kernel(tc, x, base_weight, spline_weight, out):
 
         ident = const.tile([P, P], F32, name="ident")
         make_identity(nc, ident[:])
-        minus_two = const.tile([P, P], BF16, name="minus_two")
+        twice = const.tile([P, P], F32, name="twice")
         nc.vector.tensor_scalar(
-            out=minus_two[:], in0=ident[:], scalar1=-2.0, scalar2=None, op0=ALU.mult
+            out=twice[:], in0=ident[:], scalar1=2.0, scalar2=None, op0=ALU.mult
         )
         shift = const.tile([P, 8], F32, name="shift")
         for g in range(NG):
@@ -181,74 +181,50 @@ def tile_kandense_t_kernel(tc, x, base_weight, spline_weight, out):
                     op1=ALU.mult,
                 )
 
-        def tensor_argument(c, g):
-            banks = []
-            for t in range(CHUNKS[c]):
-                if g == 4 and t == 1:
-                    break
-                for h in range(2):
-                    bank = ab_pool.tile([P, 4, P], F32, name="bank")
-                    banks.append(bank)
-                    for s in range(4):
-                        b = 8 * t + 4 * h + s
-                        sq, neg = st[c]["sq"][:, b, :], st[c]["neg"][:, b, :]
-                        terms = [sq]
-                        plain = g == 4 and t == 0
-                        if not plain:
-                            terms = terms + [neg] * (g - 2)
-                        for i, term in enumerate(terms):
-                            nc.tensor.matmul(
-                                bank[:, s, :],
-                                term,
-                                ident[:],
-                                start=(i == 0),
-                                stop=(i == len(terms) - 1 and not plain),
-                                is_transpose=True,
-                            )
-                        if plain:
-                            base = FEAT * t + 512 * h
-                            nc.tensor.matmul(
-                                bank[:, s, :],
-                                minus_two[:],
-                                st[c]["xg"][:, base : base + 512].rearrange(
-                                    "p (m s) -> p m s", s=4
-                                )[:, :, s],
-                                start=False,
-                                stop=True,
-                            )
-            st[c]["arg", g] = banks
-
-        def exponential(c, pos):
-            g = ORDER[pos]
-            n = FEAT * CHUNKS[c]
-            rg = rg_pool.tile([P, CMAX * FEAT], BF16, name="rg", align_bytes=64)
-            st[c]["rg", pos] = rg
-            bias = shift[:, g : g + 1]
-            if g in ON_VECTOR:
-                nc.scalar.activation(
-                    out=rg[:, :n],
-                    in_=st[c]["arg", g, "sbuf"][:, :n],
-                    func=AF.Exp,
-                    scale=-5.0,
-                    bias=bias,
+        def tensor_argument(c, g, q):
+            if q >= 2 * CHUNKS[c]:
+                return
+            bank = ab_pool.tile([P, 4, P], F32, name="bank")
+            st[c]["bank", g, q] = bank
+            for s in range(4):
+                sq, neg = st[c]["sq"][:, 4 * q + s, :], st[c]["neg"][:, 4 * q + s, :]
+                nc.tensor.matmul(
+                    bank[:, s, :], sq, ident[:], start=True, stop=(g == 2), is_transpose=True
                 )
-            else:
-                for q, bank in enumerate(st[c]["arg", g]):
-                    nc.scalar.activation(
-                        out=rg[:, 512 * q : 512 * q + 512].rearrange("p (m s) -> p m s", s=4),
-                        in_=bank[:].rearrange("p s m -> p m s"),
-                        func=AF.Exp,
-                        scale=-5.0,
-                        bias=bias,
+                if g == 3:
+                    nc.tensor.matmul(
+                        bank[:, s, :], neg, ident[:], start=False, stop=True, is_transpose=True
                     )
-                if g == 4 and n > FEAT:
-                    nc.scalar.activation(
-                        out=rg[:, FEAT:n],
-                        in_=st[c]["arg", g, "sbuf"][:, FEAT:n],
-                        func=AF.Exp,
-                        scale=-5.0,
-                        bias=bias,
-                    )
+                elif g == 4:
+                    nc.tensor.matmul(bank[:, s, :], neg, twice[:], start=False, stop=True)
+
+        def rbf(c, g):
+            if ("rbf", g) not in st[c]:
+                st[c]["rbf", g] = rg_pool.tile([P, CMAX * FEAT], BF16, name="rg", align_bytes=64)
+            return st[c]["rbf", g]
+
+        def exp_sbuf(c, g, first=0):
+            n = FEAT * CHUNKS[c]
+            if FEAT * first >= n:
+                return
+            nc.scalar.activation(
+                out=rbf(c, g)[:, FEAT * first : n],
+                in_=st[c]["arg", g, "sbuf"][:, FEAT * first : n],
+                func=AF.Exp,
+                scale=-5.0,
+                bias=shift[:, g : g + 1],
+            )
+
+        def exp_psum(c, g, q):
+            if q >= 2 * CHUNKS[c]:
+                return
+            nc.scalar.activation(
+                out=rbf(c, g)[:, 512 * q : 512 * q + 512].rearrange("p (m s) -> p m s", s=4),
+                in_=st[c]["bank", g, q][:].rearrange("p s m -> p m s"),
+                func=AF.Exp,
+                scale=-5.0,
+                bias=shift[:, g : g + 1],
+            )
 
         def mx_group(c, t, lo, maps):
             codes, scales, acc = st[c]["codes"], st[c]["scales"], st[c]["acc"]
@@ -315,7 +291,7 @@ def tile_kandense_t_kernel(tc, x, base_weight, spline_weight, out):
         def quantise_up_to(unit):
             while done[0] < min(unit, NG * n_chunks):
                 c, pos = divmod(done[0], NG)
-                quantise(c, 1 + ORDER[pos], st[c]["rg", pos])
+                quantise(c, 1 + ORDER[pos], st[c]["rbf", ORDER[pos]])
                 done[0] += 1
 
         load(0)
@@ -332,10 +308,11 @@ def tile_kandense_t_kernel(tc, x, base_weight, spline_weight, out):
         natural(1)
 
         for k in range(n_chunks + 2):
-            if live(k):
-                tensor_argument(k, ORDER[1])
             if live(k + 1):
                 transposes(k + 1)
+            if live(k):
+                for g, q in ((3, 0), (3, 1), (4, 0), (3, 2)):
+                    tensor_argument(k, g, q)
             if live(k + 4):
                 load(k + 4)
             quantise_up_to(NG * k - LAG if live(k) else NG * n_chunks)
@@ -350,17 +327,24 @@ def tile_kandense_t_kernel(tc, x, base_weight, spline_weight, out):
             if live(k + 1):
                 copy_x(k + 1)
             if live(k):
-                exponential(k, 0)
-                exponential(k, 1)
+                exp_sbuf(k, 1)
+                for g, q in ((3, 0), (3, 1), (4, 0), (3, 2)):
+                    exp_psum(k, g, q)
             if live(k - 2) and k != W_PERIOD:
                 products(k - 2)
+            if live(k):
+                for g, q in ((3, 3), (2, 0), (2, 1), (4, 1), (2, 2), (2, 3)):
+                    tensor_argument(k, g, q)
+                exp_psum(k, 3, 3)
+            if live(k - 2) and k != W_PERIOD:
                 half_tanh(k - 2)
             if live(k):
-                tensor_argument(k, ORDER[3])
-                exponential(k, 2)
-                exponential(k, 3)
-                tensor_argument(k, ORDER[4])
-                exponential(k, 4)
+                exp_sbuf(k, 0)
+                for g, q in ((2, 0), (2, 1), (4, 1)):
+                    exp_psum(k, g, q)
+                exp_sbuf(k, 4, 1)
+                for g, q in ((2, 2), (2, 3)):
+                    exp_psum(k, g, q)
             if k == W_PERIOD:
                 products(k - 2)
                 half_tanh(k - 2)

@@ -20,9 +20,9 @@ FLOPS = 2 * ROWS * FEAT * UNITS * MAPS
 
 CHUNKS = (1, 1) + (2,) * 22 + (1, 1)
 CMAX = 2
-ORDER = (1, 3, 0, 4, 2)
-ON_VECTOR = (1, 0)
-LAG = 1
+ORDER = (0, 3, 1, 2, 4)
+LAG = 2
+ON_SCALAR = ((0, 0), (3, 0))
 W_PERIOD = 2
 
 
@@ -34,28 +34,30 @@ def tile_kandense_t_kernel(tc, x, base_weight, spline_weight, out):
 
     with ExitStack() as ctx:
         const = ctx.enter_context(tc.tile_pool(name="const", bufs=1))
-        tok_pool = ctx.enter_context(tc.tile_pool(name="tok", bufs=3))
         xn_pool = ctx.enter_context(tc.tile_pool(name="xn", bufs=4))
         nat_pool = ctx.enter_context(tc.tile_pool(name="nat", bufs=3))
         xg_pool = ctx.enter_context(tc.tile_pool(name="xg", bufs=3))
-        arg_pool = ctx.enter_context(tc.tile_pool(name="arg", bufs=5))
-        rg_pool = ctx.enter_context(tc.tile_pool(name="rg", bufs=8))
+        arg_pool = ctx.enter_context(tc.tile_pool(name="arg", bufs=2))
+        rg_pool = ctx.enter_context(tc.tile_pool(name="rg", bufs=9))
         cd_pool = ctx.enter_context(tc.tile_pool(name="cd", bufs=3))
         ep_pool = ctx.enter_context(tc.tile_pool(name="ep", bufs=2))
-        xt_pool = ctx.enter_context(tc.psum_pool(name="xt", bufs=2))
-        ab_pool = ctx.enter_context(tc.psum_pool(name="ab", bufs=4))
+        xt_pool = ctx.enter_context(tc.psum_pool(name="xt", bufs=4))
+        ab_pool = ctx.enter_context(tc.psum_pool(name="ab", bufs=2))
         acc_pool = ctx.enter_context(tc.psum_pool(name="acc", bufs=2))
         ctx.enter_context(tc.manual_schedule())
 
         ident = const.tile([P, P], F32, name="ident")
         make_identity(nc, ident[:])
-        twice = const.tile([P, P], F32, name="twice")
+        minus_two = const.tile([P, P], BF16, name="minus_two")
         nc.vector.tensor_scalar(
-            out=twice[:], in0=ident[:], scalar1=2.0, scalar2=None, op0=ALU.mult
+            out=minus_two[:], in0=ident[:], scalar1=-2.0, scalar2=None, op0=ALU.mult
         )
         shift = const.tile([P, 8], F32, name="shift")
         for g in range(NG):
             nc.vector.memset(shift[:, g : g + 1], -5.0 * CENTRES[g] * CENTRES[g])
+        nc.vector.memset(shift[:, 5:6], 0.0)
+        for g in (0, 1):
+            nc.vector.memset(shift[:, 6 + g : 7 + g], -CENTRES[g])
         warm_in = const.tile([P, 1], F32, name="warm_in")
         warm_out = const.tile([P, 1], F32, name="warm_out")
         nc.vector.memset(warm_in[:], 0.0)
@@ -68,7 +70,6 @@ def tile_kandense_t_kernel(tc, x, base_weight, spline_weight, out):
         w_scales = const.tile([P, MAPS * 2 * UNITS], U8, name="w_scales", align_bytes=64)
 
         st = [dict() for c in range(n_chunks)]
-        token = [None]
 
         def load(c):
             n = CHUNKS[c]
@@ -110,30 +111,26 @@ def tile_kandense_t_kernel(tc, x, base_weight, spline_weight, out):
                     in_=flat[:, 4 * lo : 4 * hi],
                 )
 
-        def new_token():
-            token[0] = tok_pool.tile([P, 1], F32, name="tok")
-            nc.vector.memset(token[0][:], -1.0)
-
-        def natural(c):
-            n = CHUNKS[c]
-            src = st[c]["xn"][:, :n, :].rearrange("q t (j p e) -> q (t j) e p", j=4, e=2)
-            neg = nat_pool.tile([P, CMAX * 8, P], F32, name="neg")
-            sq = nat_pool.tile([P, CMAX * 8, P], F32, name="sq")
-            nc.gpsimd.tensor_scalar(
-                out=neg[:, : 8 * n, :].rearrange("q (a e) p -> q a e p", e=2),
-                in0=src,
-                scalar1=token[0][:],
-                scalar2=0.0,
+        def negate(c):
+            if CHUNKS[c] == 1:
+                return
+            st[c]["neg"] = nat_pool.tile([P, 8, P], F32, name="neg")
+            nc.vector.tensor_scalar(
+                out=st[c]["neg"][:].rearrange("q (j e) p -> q j e p", e=2),
+                in0=st[c]["xn"][:, 0, :].rearrange("q (j p e) -> q j e p", j=4, e=2),
+                scalar1=-1.0,
+                scalar2=None,
                 op0=ALU.mult,
-                op1=ALU.add,
             )
+
+        def square(c):
+            if CHUNKS[c] == 1:
+                return
+            st[c]["sq"] = nat_pool.tile([P, 8, P], F32, name="sq")
+            neg = st[c]["neg"][:].rearrange("q b p -> q (b p)")
             nc.gpsimd.tensor_tensor(
-                out=sq[:, : 8 * n, :].rearrange("q (a e) p -> q a e p", e=2),
-                in0=src,
-                in1=src,
-                op=ALU.mult,
+                out=st[c]["sq"][:].rearrange("q b p -> q (b p)"), in0=neg, in1=neg, op=ALU.mult
             )
-            st[c]["neg"], st[c]["sq"] = neg, sq
 
         def transposes(c):
             words = st[c]["xn"][:].bitcast(F32)
@@ -168,35 +165,60 @@ def tile_kandense_t_kernel(tc, x, base_weight, spline_weight, out):
             st[c]["scales"] = cd_pool.tile([P, MAPS, CMAX * 256], U8, name="scales", align_bytes=64)
             quantise(c, 0, st[c]["xg"])
 
-        def vector_argument(c, g, first=0):
-            arg = arg_pool.tile([P, CMAX * FEAT], F32, name="arg")
-            st[c]["arg", g, "sbuf"] = arg
-            for t in range(first, CHUNKS[c]):
-                nc.vector.scalar_tensor_tensor(
-                    out=arg[:, FEAT * t : FEAT * t + FEAT],
-                    in0=st[c]["xt"][t][:].rearrange("p m u -> p (m u)").bitcast(BF16),
-                    scalar=2.0 * CENTRES[g],
-                    in1=st[c]["xg"][:, FEAT * t : FEAT * t + FEAT],
-                    op0=ALU.subtract,
-                    op1=ALU.mult,
-                )
+        def argument_tile(c, g):
+            if ("arg", g) not in st[c]:
+                width = CMAX * FEAT if g in (0, 1) else FEAT
+                st[c]["arg", g] = arg_pool.tile([P, width], F32, name="arg" + str(g))
+            return st[c]["arg", g]
 
-        def tensor_argument(c, g, q):
-            if q >= 2 * CHUNKS[c]:
+        def argument(c, g, t):
+            lo = FEAT * t if g in (0, 1) else 0
+            return argument_tile(c, g)[:, lo : lo + FEAT]
+
+        def vector_argument(c, g, t):
+            nc.vector.scalar_tensor_tensor(
+                out=argument(c, g, t),
+                in0=st[c]["xt"][t][:].rearrange("p m u -> p (m u)").bitcast(BF16),
+                scalar=2.0 * CENTRES[g],
+                in1=st[c]["xg"][:, FEAT * t : FEAT * t + FEAT],
+                op0=ALU.subtract,
+                op1=ALU.mult,
+            )
+
+        def gpsimd_arguments(c):
+            t = CHUNKS[c] - 1
+            xg = st[c]["xg"][:, FEAT * t : FEAT * t + FEAT]
+            nc.gpsimd.tensor_tensor(out=argument(c, 2, t), in0=xg, in1=xg, op=ALU.mult)
+            nc.gpsimd.tensor_tensor(
+                out=argument(c, 3, t), in0=argument(c, 2, t), in1=xg, op=ALU.subtract
+            )
+
+        def tensor_argument(c, g):
+            if CHUNKS[c] == 1:
                 return
-            bank = ab_pool.tile([P, 4, P], F32, name="bank")
-            st[c]["bank", g, q] = bank
-            for s in range(4):
-                sq, neg = st[c]["sq"][:, 4 * q + s, :], st[c]["neg"][:, 4 * q + s, :]
-                nc.tensor.matmul(
-                    bank[:, s, :], sq, ident[:], start=True, stop=(g == 2), is_transpose=True
-                )
-                if g == 3:
+            st[c]["bank", g] = []
+            for h in range(2):
+                bank = ab_pool.tile([P, 4, P], F32, name="bank")
+                st[c]["bank", g].append(bank)
+                for s in range(4):
+                    sq, neg = st[c]["sq"][:, 4 * h + s, :], st[c]["neg"][:, 4 * h + s, :]
                     nc.tensor.matmul(
-                        bank[:, s, :], neg, ident[:], start=False, stop=True, is_transpose=True
+                        bank[:, s, :], sq, ident[:], start=True, stop=(g == 2), is_transpose=True
                     )
-                elif g == 4:
-                    nc.tensor.matmul(bank[:, s, :], neg, twice[:], start=False, stop=True)
+                    if g == 3:
+                        nc.tensor.matmul(
+                            bank[:, s, :], neg, ident[:], start=False, stop=True, is_transpose=True
+                        )
+                    elif g == 4:
+                        nc.tensor.matmul(
+                            bank[:, s, :],
+                            minus_two[:],
+                            st[c]["xg"][:, 512 * h : 512 * h + 512].rearrange(
+                                "p (m s) -> p m s", s=4
+                            )[:, :, s],
+                            start=False,
+                            stop=True,
+                        )
 
         def rbf(c, g):
             if ("rbf", g) not in st[c]:
@@ -205,26 +227,35 @@ def tile_kandense_t_kernel(tc, x, base_weight, spline_weight, out):
 
         def exp_sbuf(c, g, first=0):
             n = FEAT * CHUNKS[c]
-            if FEAT * first >= n:
-                return
+            lo = FEAT * first if CHUNKS[c] > 1 else 0
+            complete = (c, g) in ON_SCALAR
+            if complete:
+                arg = argument_tile(c, g)
+                nc.scalar.activation(
+                    out=arg[:, :n],
+                    in_=st[c]["xg"][:, :n],
+                    func=AF.Square,
+                    bias=shift[:, 6 + g : 7 + g],
+                )
             nc.scalar.activation(
-                out=rbf(c, g)[:, FEAT * first : n],
-                in_=st[c]["arg", g, "sbuf"][:, FEAT * first : n],
+                out=rbf(c, g)[:, lo:n],
+                in_=st[c]["arg", g][:, : n - lo],
                 func=AF.Exp,
                 scale=-5.0,
-                bias=shift[:, g : g + 1],
+                bias=shift[:, 5:6] if complete else shift[:, g : g + 1],
             )
 
-        def exp_psum(c, g, q):
-            if q >= 2 * CHUNKS[c]:
+        def exp_psum(c, g):
+            if CHUNKS[c] == 1:
                 return
-            nc.scalar.activation(
-                out=rbf(c, g)[:, 512 * q : 512 * q + 512].rearrange("p (m s) -> p m s", s=4),
-                in_=st[c]["bank", g, q][:].rearrange("p s m -> p m s"),
-                func=AF.Exp,
-                scale=-5.0,
-                bias=shift[:, g : g + 1],
-            )
+            for h in range(2):
+                nc.scalar.activation(
+                    out=rbf(c, g)[:, 512 * h : 512 * h + 512].rearrange("p (m s) -> p m s", s=4),
+                    in_=st[c]["bank", g][h][:].rearrange("p s m -> p m s"),
+                    func=AF.Exp,
+                    scale=-5.0,
+                    bias=shift[:, g : g + 1],
+                )
 
         def mx_group(c, t, lo, maps):
             codes, scales, acc = st[c]["codes"], st[c]["scales"], st[c]["acc"]
@@ -299,59 +330,63 @@ def tile_kandense_t_kernel(tc, x, base_weight, spline_weight, out):
         load_weights()
         load(2)
         load(3)
-        new_token()
-        natural(0)
+
+        def vector_arguments(c):
+            last = CHUNKS[c] - 1
+            work = [(g, t) for g in (0, 1) for t in range(CHUNKS[c])] + [(4, last)]
+            work = [(g, t) for g, t in work if (c, g) not in ON_SCALAR]
+            if c == 0:
+                work = [(3, 0)] + work + [(2, 0)]
+            for g, t in work:
+                vector_argument(c, g, t)
+
         transposes(0)
+        transposes(1)
         copy_x(0)
-        for g in ON_VECTOR:
-            vector_argument(0, g)
-        natural(1)
+        vector_arguments(0)
 
         for k in range(n_chunks + 2):
-            if live(k + 1):
-                transposes(k + 1)
+            if live(k + 2):
+                transposes(k + 2)
             if live(k):
-                for g, q in ((3, 0), (3, 1), (4, 0), (3, 2)):
-                    tensor_argument(k, g, q)
+                tensor_argument(k, 3)
             if live(k + 4):
                 load(k + 4)
+            if live(k + 1):
+                copy_x(k + 1)
             quantise_up_to(NG * k - LAG if live(k) else NG * n_chunks)
             if live(k):
                 quantise_x(k)
+            if live(k + 2):
+                negate(k + 2)
             if k == W_PERIOD:
                 regroup_weights()
                 quantise_weights()
-            new_token()
-            if live(k + 2):
-                natural(k + 2)
             if live(k + 1):
-                copy_x(k + 1)
+                gpsimd_arguments(k + 1)
+            if live(k + 2):
+                square(k + 2)
             if live(k):
-                exp_sbuf(k, 1)
-                for g, q in ((3, 0), (3, 1), (4, 0), (3, 2)):
-                    exp_psum(k, g, q)
+                exp_psum(k, 3)
+                exp_sbuf(k, 0)
             if live(k - 2) and k != W_PERIOD:
                 products(k - 2)
             if live(k):
-                for g, q in ((3, 3), (2, 0), (2, 1), (4, 1), (2, 2), (2, 3)):
-                    tensor_argument(k, g, q)
-                exp_psum(k, 3, 3)
+                tensor_argument(k, 2)
+                exp_psum(k, 2)
+                exp_sbuf(k, 3, 1)
             if live(k - 2) and k != W_PERIOD:
                 half_tanh(k - 2)
             if live(k):
-                exp_sbuf(k, 0)
-                for g, q in ((2, 0), (2, 1), (4, 1)):
-                    exp_psum(k, g, q)
+                tensor_argument(k, 4)
+                exp_sbuf(k, 1)
+                exp_psum(k, 4)
+                exp_sbuf(k, 2, 1)
                 exp_sbuf(k, 4, 1)
-                for g, q in ((2, 2), (2, 3)):
-                    exp_psum(k, g, q)
             if k == W_PERIOD:
                 products(k - 2)
                 half_tanh(k - 2)
             if live(k + 1):
-                for g in ON_VECTOR:
-                    vector_argument(k + 1, g)
-                if CHUNKS[k + 1] > 1:
-                    vector_argument(k + 1, 4, 1)
+                vector_arguments(k + 1)
             if live(k - 2):
                 finish(k - 2)

@@ -22,7 +22,8 @@ CHUNKS = (1, 1) + (2,) * 22 + (1, 1)
 CMAX = 2
 ORDER = (0, 3, 1, 2, 4)
 LAG = 2
-ON_SCALAR = ((0, 0), (3, 0))
+ON_SCALAR = ((0, 0), (0, 1), (1, 0), (1, 1), (3, 0))
+WITHOUT_GPSIMD = (0, 1)
 W_PERIOD = 2
 
 
@@ -144,13 +145,13 @@ def tile_kandense_t_kernel(tc, x, base_weight, spline_weight, out):
                         xt[:, P * h : P * h + P, u], words[:, t, P * j : P * j + P], ident[:]
                     )
 
-        def copy_x(c):
-            st[c]["xg"] = xg_pool.tile([P, CMAX * FEAT], BF16, name="xg", align_bytes=64)
-            for t in range(CHUNKS[c]):
-                nc.vector.tensor_copy(
-                    out=st[c]["xg"][:].bitcast(F32)[:, 512 * t : 512 * t + 512],
-                    in_=st[c]["xt"][t][:].rearrange("p m u -> p (m u)"),
-                )
+        def copy_x(c, t):
+            if "xg" not in st[c]:
+                st[c]["xg"] = xg_pool.tile([P, CMAX * FEAT], BF16, name="xg", align_bytes=64)
+            nc.vector.tensor_copy(
+                out=st[c]["xg"][:].bitcast(F32)[:, 512 * t : 512 * t + 512],
+                in_=st[c]["xt"][t][:].rearrange("p m u -> p (m u)"),
+            )
 
         def quantise(c, m, src):
             n = CHUNKS[c]
@@ -175,22 +176,31 @@ def tile_kandense_t_kernel(tc, x, base_weight, spline_weight, out):
             lo = FEAT * t if g in (0, 1) else 0
             return argument_tile(c, g)[:, lo : lo + FEAT]
 
-        def vector_argument(c, g, t):
+        def vector_argument(c, g, t, lo=0):
             nc.vector.scalar_tensor_tensor(
-                out=argument(c, g, t),
-                in0=st[c]["xt"][t][:].rearrange("p m u -> p (m u)").bitcast(BF16),
+                out=argument(c, g, t)[:, lo:],
+                in0=st[c]["xt"][t][:].rearrange("p m u -> p (m u)").bitcast(BF16)[:, lo:],
                 scalar=2.0 * CENTRES[g],
-                in1=st[c]["xg"][:, FEAT * t : FEAT * t + FEAT],
+                in1=st[c]["xg"][:, FEAT * t + lo : FEAT * t + FEAT],
                 op0=ALU.subtract,
                 op1=ALU.mult,
             )
 
-        def gpsimd_arguments(c):
+        def last_xg(c):
             t = CHUNKS[c] - 1
-            xg = st[c]["xg"][:, FEAT * t : FEAT * t + FEAT]
-            nc.gpsimd.tensor_tensor(out=argument(c, 2, t), in0=xg, in1=xg, op=ALU.mult)
+            return st[c]["xg"][:, FEAT * t : FEAT * t + FEAT]
+
+        def gpsimd_square(c):
+            arg = argument(c, 2, CHUNKS[c] - 1)
+            nc.gpsimd.tensor_tensor(out=arg, in0=last_xg(c), in1=last_xg(c), op=ALU.mult)
+
+        def gpsimd_difference(c):
+            t = CHUNKS[c] - 1
             nc.gpsimd.tensor_tensor(
-                out=argument(c, 3, t), in0=argument(c, 2, t), in1=xg, op=ALU.subtract
+                out=argument(c, 3, t)[:, :768],
+                in0=argument(c, 2, t)[:, :768],
+                in1=last_xg(c)[:, :768],
+                op=ALU.subtract,
             )
 
         def tensor_argument(c, g):
@@ -287,23 +297,26 @@ def tile_kandense_t_kernel(tc, x, base_weight, spline_weight, out):
                 out=st[c]["th"][:, :w], in_=st[c]["acc"][:, :w], func=AF.Tanh, scale=0.5
             )
 
+        def silu_twice(c):
+            w = UNITS * CHUNKS[c]
+            st[c]["s2"] = ep_pool.tile([P, UNITS * CMAX], F32, name="s2")
+            nc.vector.scalar_tensor_tensor(
+                out=st[c]["s2"][:, :w],
+                in0=st[c]["th"][:, :w],
+                scalar=1.0,
+                in1=st[c]["acc"][:, :w],
+                op0=ALU.add,
+                op1=ALU.mult,
+            )
+
         def finish(c):
             n = CHUNKS[c]
             w = UNITS * n
             acc = st[c]["acc"]
-            s2 = ep_pool.tile([P, UNITS * CMAX], F32, name="s2")
-            nc.vector.scalar_tensor_tensor(
-                out=s2[:, :w],
-                in0=st[c]["th"][:, :w],
-                scalar=1.0,
-                in1=acc[:, :w],
-                op0=ALU.add,
-                op1=ALU.mult,
-            )
             res = ep_pool.tile([P, UNITS * CMAX], F32, name="res")
             nc.vector.scalar_tensor_tensor(
                 out=res[:, :w],
-                in0=s2[:, :w],
+                in0=st[c]["s2"][:, :w],
                 scalar=0.5,
                 in1=acc[:, 256 : 256 + w],
                 op0=ALU.mult,
@@ -327,33 +340,39 @@ def tile_kandense_t_kernel(tc, x, base_weight, spline_weight, out):
 
         load(0)
         load(1)
-        load_weights()
         load(2)
+        load_weights()
         load(3)
 
         def vector_arguments(c):
             last = CHUNKS[c] - 1
             work = [(g, t) for g in (0, 1) for t in range(CHUNKS[c])] + [(4, last)]
             work = [(g, t) for g, t in work if (c, g) not in ON_SCALAR]
-            if c == 0:
+            if c in WITHOUT_GPSIMD:
                 work = [(3, 0)] + work + [(2, 0)]
             for g, t in work:
                 vector_argument(c, g, t)
+            if c not in WITHOUT_GPSIMD and 768 < FEAT:
+                vector_argument(c, 3, last, 768)
 
         transposes(0)
         transposes(1)
-        copy_x(0)
+        copy_x(0, 0)
         vector_arguments(0)
 
         for k in range(n_chunks + 2):
-            if live(k + 2):
-                transposes(k + 2)
             if live(k):
                 tensor_argument(k, 3)
             if live(k + 4):
                 load(k + 4)
+            if live(k - 3) and k <= n_chunks:
+                silu_twice(k - 3)
+            if live(k + 1) and CHUNKS[k + 1] > 1:
+                copy_x(k + 1, 0)
+            if live(k - 3) and k <= n_chunks:
+                finish(k - 3)
             if live(k + 1):
-                copy_x(k + 1)
+                copy_x(k + 1, CHUNKS[k + 1] - 1)
             quantise_up_to(NG * k - LAG if live(k) else NG * n_chunks)
             if live(k):
                 quantise_x(k)
@@ -362,25 +381,30 @@ def tile_kandense_t_kernel(tc, x, base_weight, spline_weight, out):
             if k == W_PERIOD:
                 regroup_weights()
                 quantise_weights()
-            if live(k + 1):
-                gpsimd_arguments(k + 1)
             if live(k + 2):
                 square(k + 2)
+            if live(k + 1) and k + 1 not in WITHOUT_GPSIMD:
+                gpsimd_square(k + 1)
+                gpsimd_difference(k + 1)
             if live(k):
                 exp_psum(k, 3)
                 exp_sbuf(k, 0)
-            if live(k - 2) and k != W_PERIOD:
-                products(k - 2)
             if live(k):
                 tensor_argument(k, 2)
                 exp_psum(k, 2)
                 exp_sbuf(k, 3, 1)
             if live(k - 2) and k != W_PERIOD:
-                half_tanh(k - 2)
+                products(k - 2)
             if live(k):
                 tensor_argument(k, 4)
+            if live(k + 2):
+                transposes(k + 2)
+            if live(k):
                 exp_sbuf(k, 1)
                 exp_psum(k, 4)
+            if live(k - 2) and k != W_PERIOD:
+                half_tanh(k - 2)
+            if live(k):
                 exp_sbuf(k, 2, 1)
                 exp_sbuf(k, 4, 1)
             if k == W_PERIOD:
@@ -388,5 +412,6 @@ def tile_kandense_t_kernel(tc, x, base_weight, spline_weight, out):
                 half_tanh(k - 2)
             if live(k + 1):
                 vector_arguments(k + 1)
-            if live(k - 2):
+            if k >= n_chunks and live(k - 2):
+                silu_twice(k - 2)
                 finish(k - 2)

@@ -21,8 +21,9 @@ FLOPS = 2 * ROWS * FEAT * UNITS * MAPS
 CHUNKS = (1, 1) + (2,) * 22 + (1, 1)
 CMAX = 2
 ORDER = (0, 3, 1, 2, 4)
-LAG = 2
-ON_SCALAR = ((0, 0), (0, 1), (1, 0), (1, 1), (3, 0))
+LAG = 1
+EXTRA = (0, 2, 4)
+ON_SCALAR = ((0, 0), (0, 1), (1, 0), (1, 1))
 WITHOUT_GPSIMD = (0, 1)
 W_PERIOD = 2
 
@@ -42,17 +43,23 @@ def tile_kandense_t_kernel(tc, x, base_weight, spline_weight, out):
         rg_pool = ctx.enter_context(tc.tile_pool(name="rg", bufs=9))
         cd_pool = ctx.enter_context(tc.tile_pool(name="cd", bufs=3))
         ep_pool = ctx.enter_context(tc.tile_pool(name="ep", bufs=2))
-        xt_pool = ctx.enter_context(tc.psum_pool(name="xt", bufs=4))
-        ab_pool = ctx.enter_context(tc.psum_pool(name="ab", bufs=2))
+        xt_pool = ctx.enter_context(tc.psum_pool(name="xt", bufs=3))
+        ab_pool = ctx.enter_context(tc.psum_pool(name="ab", bufs=3))
         acc_pool = ctx.enter_context(tc.psum_pool(name="acc", bufs=2))
         ctx.enter_context(tc.manual_schedule())
 
         ident = const.tile([P, P], F32, name="ident")
         make_identity(nc, ident[:])
-        minus_two = const.tile([P, P], BF16, name="minus_two")
-        nc.vector.tensor_scalar(
-            out=minus_two[:], in0=ident[:], scalar1=-2.0, scalar2=None, op0=ALU.mult
-        )
+        factor = {}
+        for g in (1, 4):
+            factor[g] = const.tile([P, P], BF16, name="factor" + str(g))
+            nc.vector.tensor_scalar(
+                out=factor[g][:],
+                in0=ident[:],
+                scalar1=-2.0 * CENTRES[g],
+                scalar2=None,
+                op0=ALU.mult,
+            )
         shift = const.tile([P, 8], F32, name="shift")
         for g in range(NG):
             nc.vector.memset(shift[:, g : g + 1], -5.0 * CENTRES[g] * CENTRES[g])
@@ -176,6 +183,9 @@ def tile_kandense_t_kernel(tc, x, base_weight, spline_weight, out):
             lo = FEAT * t if g in (0, 1) else 0
             return argument_tile(c, g)[:, lo : lo + FEAT]
 
+        def on_tensor(c):
+            return 512 if CHUNKS[c] > 1 and c % 5 in EXTRA else 0
+
         def vector_argument(c, g, t, lo=0):
             nc.vector.scalar_tensor_tensor(
                 out=argument(c, g, t)[:, lo:],
@@ -197,17 +207,17 @@ def tile_kandense_t_kernel(tc, x, base_weight, spline_weight, out):
         def gpsimd_difference(c):
             t = CHUNKS[c] - 1
             nc.gpsimd.tensor_tensor(
-                out=argument(c, 3, t)[:, :768],
-                in0=argument(c, 2, t)[:, :768],
-                in1=last_xg(c)[:, :768],
+                out=argument(c, 3, t)[:, :512],
+                in0=argument(c, 2, t)[:, :512],
+                in1=last_xg(c)[:, :512],
                 op=ALU.subtract,
             )
 
-        def tensor_argument(c, g):
+        def tensor_argument(c, g, halves=(0, 1)):
             if CHUNKS[c] == 1:
                 return
             st[c]["bank", g] = []
-            for h in range(2):
+            for h in halves:
                 bank = ab_pool.tile([P, 4, P], F32, name="bank")
                 st[c]["bank", g].append(bank)
                 for s in range(4):
@@ -219,10 +229,10 @@ def tile_kandense_t_kernel(tc, x, base_weight, spline_weight, out):
                         nc.tensor.matmul(
                             bank[:, s, :], neg, ident[:], start=False, stop=True, is_transpose=True
                         )
-                    elif g == 4:
+                    elif g in (1, 4):
                         nc.tensor.matmul(
                             bank[:, s, :],
-                            minus_two[:],
+                            factor[g][:],
                             st[c]["xg"][:, 512 * h : 512 * h + 512].rearrange(
                                 "p (m s) -> p m s", s=4
                             )[:, :, s],
@@ -235,7 +245,7 @@ def tile_kandense_t_kernel(tc, x, base_weight, spline_weight, out):
                 st[c]["rbf", g] = rg_pool.tile([P, CMAX * FEAT], BF16, name="rg", align_bytes=64)
             return st[c]["rbf", g]
 
-        def exp_sbuf(c, g, first=0):
+        def exp_sbuf(c, g, first=0, skip=0):
             n = FEAT * CHUNKS[c]
             lo = FEAT * first if CHUNKS[c] > 1 else 0
             complete = (c, g) in ON_SCALAR
@@ -248,8 +258,8 @@ def tile_kandense_t_kernel(tc, x, base_weight, spline_weight, out):
                     bias=shift[:, 6 + g : 7 + g],
                 )
             nc.scalar.activation(
-                out=rbf(c, g)[:, lo:n],
-                in_=st[c]["arg", g][:, : n - lo],
+                out=rbf(c, g)[:, lo + skip : n],
+                in_=st[c]["arg", g][:, skip : n - lo],
                 func=AF.Exp,
                 scale=-5.0,
                 bias=shift[:, 5:6] if complete else shift[:, g : g + 1],
@@ -258,10 +268,10 @@ def tile_kandense_t_kernel(tc, x, base_weight, spline_weight, out):
         def exp_psum(c, g):
             if CHUNKS[c] == 1:
                 return
-            for h in range(2):
+            for h, bank in enumerate(st[c]["bank", g]):
                 nc.scalar.activation(
                     out=rbf(c, g)[:, 512 * h : 512 * h + 512].rearrange("p (m s) -> p m s", s=4),
-                    in_=st[c]["bank", g][h][:].rearrange("p s m -> p m s"),
+                    in_=bank[:].rearrange("p s m -> p m s"),
                     func=AF.Exp,
                     scale=-5.0,
                     bias=shift[:, g : g + 1],
@@ -351,9 +361,9 @@ def tile_kandense_t_kernel(tc, x, base_weight, spline_weight, out):
             if c in WITHOUT_GPSIMD:
                 work = [(3, 0)] + work + [(2, 0)]
             for g, t in work:
-                vector_argument(c, g, t)
-            if c not in WITHOUT_GPSIMD and 768 < FEAT:
-                vector_argument(c, 3, last, 768)
+                vector_argument(c, g, t, on_tensor(c) if (g, t) == (1, 0) else 0)
+            if c not in WITHOUT_GPSIMD and 512 < FEAT:
+                vector_argument(c, 3, last, 512)
 
         transposes(0)
         transposes(1)
@@ -363,13 +373,16 @@ def tile_kandense_t_kernel(tc, x, base_weight, spline_weight, out):
         for k in range(n_chunks + 2):
             if live(k):
                 tensor_argument(k, 3)
+            if k == W_PERIOD + 1:
+                products(k - 3)
             if live(k + 4):
                 load(k + 4)
-            if live(k - 3) and k <= n_chunks:
+            settle = live(k - 3) and k <= n_chunks
+            if settle and k != W_PERIOD + 1:
                 silu_twice(k - 3)
             if live(k + 1) and CHUNKS[k + 1] > 1:
                 copy_x(k + 1, 0)
-            if live(k - 3) and k <= n_chunks:
+            if settle and k != W_PERIOD + 1:
                 finish(k - 3)
             if live(k + 1):
                 copy_x(k + 1, CHUNKS[k + 1] - 1)
@@ -393,6 +406,8 @@ def tile_kandense_t_kernel(tc, x, base_weight, spline_weight, out):
                 tensor_argument(k, 2)
                 exp_psum(k, 2)
                 exp_sbuf(k, 3, 1)
+            if live(k) and on_tensor(k) > 0:
+                tensor_argument(k, 1, (0,))
             if live(k - 2) and k != W_PERIOD:
                 products(k - 2)
             if live(k):
@@ -400,18 +415,22 @@ def tile_kandense_t_kernel(tc, x, base_weight, spline_weight, out):
             if live(k + 2):
                 transposes(k + 2)
             if live(k):
-                exp_sbuf(k, 1)
+                if on_tensor(k) > 0:
+                    exp_psum(k, 1)
+                exp_sbuf(k, 1, 0, on_tensor(k))
                 exp_psum(k, 4)
             if live(k - 2) and k != W_PERIOD:
                 half_tanh(k - 2)
             if live(k):
                 exp_sbuf(k, 2, 1)
                 exp_sbuf(k, 4, 1)
-            if k == W_PERIOD:
-                products(k - 2)
-                half_tanh(k - 2)
+            if k == W_PERIOD + 1:
+                half_tanh(k - 3)
             if live(k + 1):
                 vector_arguments(k + 1)
+            if k == W_PERIOD + 1:
+                silu_twice(k - 3)
+                finish(k - 3)
             if k >= n_chunks and live(k - 2):
                 silu_twice(k - 2)
                 finish(k - 2)

@@ -20,12 +20,13 @@ FLOPS = 2 * ROWS * FEAT * UNITS * MAPS
 
 CHUNKS = (1, 1) + (2,) * 22 + (1, 1)
 CMAX = 2
-ORDER = (0, 3, 1, 2, 4)
+GROUPS = ((0, 3), (1, 2), (4,))
+SLOT = {-1: 0, 0: 1, 3: 2, 1: 3, 2: 4, 4: 5}
 LAG = 1
-EXTRA = (0, 2, 4)
 ON_SCALAR = ((0, 0), (0, 1), (1, 0), (1, 1))
 WITHOUT_GPSIMD = (0, 1)
 W_PERIOD = 2
+SHARE = 896
 
 
 def tile_kandense_t_kernel(tc, x, base_weight, spline_weight, out):
@@ -38,9 +39,9 @@ def tile_kandense_t_kernel(tc, x, base_weight, spline_weight, out):
         const = ctx.enter_context(tc.tile_pool(name="const", bufs=1))
         xn_pool = ctx.enter_context(tc.tile_pool(name="xn", bufs=4))
         nat_pool = ctx.enter_context(tc.tile_pool(name="nat", bufs=3))
-        xg_pool = ctx.enter_context(tc.tile_pool(name="xg", bufs=3))
+        xg_pool = ctx.enter_context(tc.tile_pool(name="xg", bufs=2))
         arg_pool = ctx.enter_context(tc.tile_pool(name="arg", bufs=2))
-        rg_pool = ctx.enter_context(tc.tile_pool(name="rg", bufs=9))
+        rg_pool = ctx.enter_context(tc.tile_pool(name="rg", bufs=2))
         cd_pool = ctx.enter_context(tc.tile_pool(name="cd", bufs=3))
         ep_pool = ctx.enter_context(tc.tile_pool(name="ep", bufs=2))
         xt_pool = ctx.enter_context(tc.psum_pool(name="xt", bufs=3))
@@ -66,10 +67,8 @@ def tile_kandense_t_kernel(tc, x, base_weight, spline_weight, out):
         nc.vector.memset(shift[:, 5:6], 0.0)
         for g in (0, 1):
             nc.vector.memset(shift[:, 6 + g : 7 + g], -CENTRES[g])
-        warm_in = const.tile([P, 1], F32, name="warm_in")
         warm_out = const.tile([P, 1], F32, name="warm_out")
-        nc.vector.memset(warm_in[:], 0.0)
-        nc.scalar.activation(out=warm_out[:], in_=warm_in[:], func=AF.Exp)
+        nc.scalar.activation(out=warm_out[:], in_=shift[:, 5:6], func=AF.Exp)
 
         wb_raw = const.tile([P, 4, 2 * UNITS], BF16, name="wb_raw")
         ws_raw = const.tile([P, 4, 2 * UNITS * 8], BF16, name="ws_raw")
@@ -160,18 +159,19 @@ def tile_kandense_t_kernel(tc, x, base_weight, spline_weight, out):
                 in_=st[c]["xt"][t][:].rearrange("p m u -> p (m u)"),
             )
 
-        def quantise(c, m, src):
+        def quantise(c, slot, maps, src):
             n = CHUNKS[c]
+            words = slice(256 * n * slot, 256 * n * (slot + maps))
             nc.vector.quantize_mx(
-                out=st[c]["codes"][:, m, : 256 * n].bitcast(FP8X4),
-                scales=st[c]["scales"][:, m, : 256 * n],
-                in_=src[:, : FEAT * n],
+                out=st[c]["codes"][:, words].bitcast(FP8X4),
+                scales=st[c]["scales"][:, words],
+                in_=src[:, : FEAT * n * maps],
             )
 
         def quantise_x(c):
-            st[c]["codes"] = cd_pool.tile([P, MAPS, CMAX * 256], U32, name="codes", align_bytes=64)
-            st[c]["scales"] = cd_pool.tile([P, MAPS, CMAX * 256], U8, name="scales", align_bytes=64)
-            quantise(c, 0, st[c]["xg"])
+            st[c]["codes"] = cd_pool.tile([P, MAPS * CMAX * 256], U32, name="codes", align_bytes=64)
+            st[c]["scales"] = cd_pool.tile([P, MAPS * CMAX * 256], U8, name="scales", align_bytes=64)
+            quantise(c, 0, 1, st[c]["xg"])
 
         def argument_tile(c, g):
             if ("arg", g) not in st[c]:
@@ -184,7 +184,7 @@ def tile_kandense_t_kernel(tc, x, base_weight, spline_weight, out):
             return argument_tile(c, g)[:, lo : lo + FEAT]
 
         def on_tensor(c):
-            return 512 if CHUNKS[c] > 1 and c % 5 in EXTRA else 0
+            return 512 if CHUNKS[c] > 1 and c % 5 in (0, 2, 4) else 0
 
         def vector_argument(c, g, t, lo=0):
             nc.vector.scalar_tensor_tensor(
@@ -207,9 +207,9 @@ def tile_kandense_t_kernel(tc, x, base_weight, spline_weight, out):
         def gpsimd_difference(c):
             t = CHUNKS[c] - 1
             nc.gpsimd.tensor_tensor(
-                out=argument(c, 3, t)[:, :512],
-                in0=argument(c, 2, t)[:, :512],
-                in1=last_xg(c)[:, :512],
+                out=argument(c, 3, t)[:, :SHARE],
+                in0=argument(c, 2, t)[:, :SHARE],
+                in1=last_xg(c)[:, :SHARE],
                 op=ALU.subtract,
             )
 
@@ -241,9 +241,15 @@ def tile_kandense_t_kernel(tc, x, base_weight, spline_weight, out):
                         )
 
         def rbf(c, g):
-            if ("rbf", g) not in st[c]:
-                st[c]["rbf", g] = rg_pool.tile([P, CMAX * FEAT], BF16, name="rg", align_bytes=64)
-            return st[c]["rbf", g]
+            for i, group in enumerate(GROUPS):
+                if g in group:
+                    if ("rg", i) not in st[c]:
+                        st[c]["rg", i] = rg_pool.tile(
+                            [P, len(group) * CMAX * FEAT], BF16, name="rg" + str(i), align_bytes=64
+                        )
+                    n = FEAT * CHUNKS[c]
+                    lo = n * group.index(g)
+                    return st[c]["rg", i][:, lo : lo + n]
 
         def exp_sbuf(c, g, first=0, skip=0):
             n = FEAT * CHUNKS[c]
@@ -277,16 +283,17 @@ def tile_kandense_t_kernel(tc, x, base_weight, spline_weight, out):
                     bias=shift[:, g : g + 1],
                 )
 
-        def mx_group(c, t, lo, maps):
-            codes, scales, acc = st[c]["codes"], st[c]["scales"], st[c]["acc"]
-            steps = [(m, h) for m in maps for h in range(2)]
-            for i, (m, h) in enumerate(steps):
-                a = slice(P * (2 * t + h), P * (2 * t + h) + P)
-                b = slice(P * (2 * m + h), P * (2 * m + h) + P)
+        def mx_group(c, t, lo, centres):
+            codes, scales, acc, n = st[c]["codes"], st[c]["scales"], st[c]["acc"], CHUNKS[c]
+            steps = [(g, h) for g in centres for h in range(2)]
+            for i, (g, h) in enumerate(steps):
+                col = 256 * n * SLOT[g] + P * (2 * t + h)
+                a = slice(col, col + P)
+                b = slice(P * (2 * (g + 1) + h), P * (2 * (g + 1) + h) + P)
                 nc.tensor.matmul_mx(
                     out=acc[:, lo + P * t : lo + P * t + P],
-                    lhsT=codes[:, m, a].bitcast(FP8X4),
-                    lhsT_scale=scales[:, m, a],
+                    lhsT=codes[:, a].bitcast(FP8X4),
+                    lhsT_scale=scales[:, a],
                     rhs=w_codes[:, b].bitcast(FP8X4),
                     rhs_scale=w_scales[:, b],
                     start=(i == 0),
@@ -296,9 +303,9 @@ def tile_kandense_t_kernel(tc, x, base_weight, spline_weight, out):
         def products(c):
             st[c]["acc"] = acc_pool.tile([P, 512], F32, name="acc")
             for t in range(CHUNKS[c]):
-                mx_group(c, t, 0, [0])
+                mx_group(c, t, 0, [-1])
             for t in range(CHUNKS[c]):
-                mx_group(c, t, 256, [1 + g for g in ORDER])
+                mx_group(c, t, 256, [g for group in GROUPS for g in group])
 
         def half_tanh(c):
             w = UNITS * CHUNKS[c]
@@ -322,13 +329,12 @@ def tile_kandense_t_kernel(tc, x, base_weight, spline_weight, out):
         def finish(c):
             n = CHUNKS[c]
             w = UNITS * n
-            acc = st[c]["acc"]
             res = ep_pool.tile([P, UNITS * CMAX], F32, name="res")
             nc.vector.scalar_tensor_tensor(
                 out=res[:, :w],
                 in0=st[c]["s2"][:, :w],
                 scalar=0.5,
-                in1=acc[:, 256 : 256 + w],
+                in1=st[c]["acc"][:, 256 : 256 + w],
                 op0=ALU.mult,
                 op1=ALU.add,
             )
@@ -343,50 +349,47 @@ def tile_kandense_t_kernel(tc, x, base_weight, spline_weight, out):
         done = [0]
 
         def quantise_up_to(unit):
-            while done[0] < min(unit, NG * n_chunks):
-                c, pos = divmod(done[0], NG)
-                quantise(c, 1 + ORDER[pos], st[c]["rbf", ORDER[pos]])
+            while done[0] < min(unit, len(GROUPS) * n_chunks):
+                c, i = divmod(done[0], len(GROUPS))
+                quantise(c, SLOT[GROUPS[i][0]], len(GROUPS[i]), st[c]["rg", i])
                 done[0] += 1
-
-        load(0)
-        load(1)
-        load(2)
-        load_weights()
-        load(3)
 
         def vector_arguments(c):
             last = CHUNKS[c] - 1
             work = [(g, t) for g in (0, 1) for t in range(CHUNKS[c])] + [(4, last)]
             work = [(g, t) for g, t in work if (c, g) not in ON_SCALAR]
             if c in WITHOUT_GPSIMD:
-                work = [(3, 0)] + work + [(2, 0)]
+                work = [(3, 0), (2, 0)] + work
             for g, t in work:
                 vector_argument(c, g, t, on_tensor(c) if (g, t) == (1, 0) else 0)
-            if c not in WITHOUT_GPSIMD and 512 < FEAT:
-                vector_argument(c, 3, last, 512)
+            if c not in WITHOUT_GPSIMD and SHARE < FEAT:
+                vector_argument(c, 3, last, SHARE)
 
+        load(0)
+        load(1)
+        load(2)
+        load_weights()
+        load(3)
         transposes(0)
         transposes(1)
         copy_x(0, 0)
         vector_arguments(0)
 
         for k in range(n_chunks + 2):
-            if live(k):
-                tensor_argument(k, 3)
             if k == W_PERIOD + 1:
                 products(k - 3)
             if live(k + 4):
                 load(k + 4)
-            settle = live(k - 3) and k <= n_chunks
-            if settle and k != W_PERIOD + 1:
+            settle = live(k - 3) and k <= n_chunks and k != W_PERIOD + 1
+            if settle:
                 silu_twice(k - 3)
             if live(k + 1) and CHUNKS[k + 1] > 1:
                 copy_x(k + 1, 0)
-            if settle and k != W_PERIOD + 1:
+            if settle:
                 finish(k - 3)
             if live(k + 1):
                 copy_x(k + 1, CHUNKS[k + 1] - 1)
-            quantise_up_to(NG * k - LAG if live(k) else NG * n_chunks)
+            quantise_up_to(len(GROUPS) * k - LAG if live(k) else len(GROUPS) * n_chunks)
             if live(k):
                 quantise_x(k)
             if live(k + 2):
@@ -402,7 +405,6 @@ def tile_kandense_t_kernel(tc, x, base_weight, spline_weight, out):
             if live(k):
                 exp_psum(k, 3)
                 exp_sbuf(k, 0)
-            if live(k):
                 tensor_argument(k, 2)
                 exp_psum(k, 2)
                 exp_sbuf(k, 3, 1)
@@ -412,6 +414,8 @@ def tile_kandense_t_kernel(tc, x, base_weight, spline_weight, out):
                 products(k - 2)
             if live(k):
                 tensor_argument(k, 4)
+            if live(k + 1):
+                tensor_argument(k + 1, 3)
             if live(k + 2):
                 transposes(k + 2)
             if live(k):

@@ -26,7 +26,7 @@ LAG = 1
 ON_SCALAR = ((0, 0), (0, 1), (1, 0), (1, 1))
 WITHOUT_GPSIMD = (0, 1)
 W_PERIOD = 2
-SHARE = 896
+SHARE = 768
 
 
 def tile_kandense_t_kernel(tc, x, base_weight, spline_weight, out):
@@ -43,7 +43,7 @@ def tile_kandense_t_kernel(tc, x, base_weight, spline_weight, out):
         arg_pool = ctx.enter_context(tc.tile_pool(name="arg", bufs=2))
         rg_pool = ctx.enter_context(tc.tile_pool(name="rg", bufs=2))
         cd_pool = ctx.enter_context(tc.tile_pool(name="cd", bufs=3))
-        ep_pool = ctx.enter_context(tc.tile_pool(name="ep", bufs=2))
+        ep_pool = ctx.enter_context(tc.tile_pool(name="ep", bufs=3))
         xt_pool = ctx.enter_context(tc.psum_pool(name="xt", bufs=3))
         ab_pool = ctx.enter_context(tc.psum_pool(name="ab", bufs=3))
         acc_pool = ctx.enter_context(tc.psum_pool(name="acc", bufs=2))
@@ -98,16 +98,13 @@ def tile_kandense_t_kernel(tc, x, base_weight, spline_weight, out):
 
         def regroup_weights():
             for m in range(MAPS):
-                for h in range(2):
-                    if m == 0:
-                        src = wb_raw[:, 2 * h : 2 * h + 2, :].rearrange("p u (e c) -> p c u e", e=2)
-                    else:
-                        src = ws_raw[:, 2 * h : 2 * h + 2, :].rearrange(
-                            "p u (e c s) -> p c u e s", e=2, s=8
-                        )[:, :, :, :, m - 1]
-                    nc.vector.tensor_copy(
-                        out=w_grouped[:, m, h].rearrange("p c (u e) -> p c u e", u=2), in_=src
-                    )
+                if m == 0:
+                    src = wb_raw[:].rearrange("p a (e c) -> p (a e) c", e=2)
+                else:
+                    src = ws_raw[:].rearrange("p a (e c s) -> p (a e) c s", e=2, s=8)[:, :, :, m - 1]
+                nc.vector.tensor_copy(
+                    out=w_grouped[:, m], in_=src.rearrange("p (h t) c -> p h c t", h=2)
+                )
 
         def quantise_weights():
             flat = w_grouped[:].rearrange("p m h c t -> p (m h c t)")
@@ -184,7 +181,12 @@ def tile_kandense_t_kernel(tc, x, base_weight, spline_weight, out):
             return argument_tile(c, g)[:, lo : lo + FEAT]
 
         def on_tensor(c):
-            return 512 if CHUNKS[c] > 1 and c % 5 in (0, 2, 4) else 0
+            return 512 if CHUNKS[c] > 1 else 0
+
+        def by_transposes(c, g, h):
+            if g == 4:
+                return 2 if h == 0 and c % 5 in (1, 3) else 0
+            return 1 if g == 3 else 0
 
         def vector_argument(c, g, t, lo=0):
             nc.vector.scalar_tensor_tensor(
@@ -225,11 +227,12 @@ def tile_kandense_t_kernel(tc, x, base_weight, spline_weight, out):
                     nc.tensor.matmul(
                         bank[:, s, :], sq, ident[:], start=True, stop=(g == 2), is_transpose=True
                     )
-                    if g == 3:
+                    repeat = by_transposes(c, g, h)
+                    for i in range(repeat):
                         nc.tensor.matmul(
-                            bank[:, s, :], neg, ident[:], start=False, stop=True, is_transpose=True
+                            bank[:, s, :], neg, ident[:], start=False, stop=(i == repeat - 1), is_transpose=True
                         )
-                    elif g in (1, 4):
+                    if g in (1, 4) and repeat == 0:
                         nc.tensor.matmul(
                             bank[:, s, :],
                             factor[g][:],
@@ -283,15 +286,15 @@ def tile_kandense_t_kernel(tc, x, base_weight, spline_weight, out):
                     bias=shift[:, g : g + 1],
                 )
 
-        def mx_group(c, t, lo, centres):
-            codes, scales, acc, n = st[c]["codes"], st[c]["scales"], st[c]["acc"], CHUNKS[c]
+        def mx_group(c, t, acc, centres):
+            codes, scales, n = st[c]["codes"], st[c]["scales"], CHUNKS[c]
             steps = [(g, h) for g in centres for h in range(2)]
             for i, (g, h) in enumerate(steps):
                 col = 256 * n * SLOT[g] + P * (2 * t + h)
                 a = slice(col, col + P)
                 b = slice(P * (2 * (g + 1) + h), P * (2 * (g + 1) + h) + P)
                 nc.tensor.matmul_mx(
-                    out=acc[:, lo + P * t : lo + P * t + P],
+                    out=acc[:, P * t : P * t + P],
                     lhsT=codes[:, a].bitcast(FP8X4),
                     lhsT_scale=scales[:, a],
                     rhs=w_codes[:, b].bitcast(FP8X4),
@@ -300,18 +303,26 @@ def tile_kandense_t_kernel(tc, x, base_weight, spline_weight, out):
                     stop=(i == len(steps) - 1),
                 )
 
+        def base_product(c, acc):
+            st[c]["base"] = acc[:, : UNITS * CHUNKS[c]]
+            for t in range(CHUNKS[c]):
+                mx_group(c, t, st[c]["base"], [-1])
+
+        def spline_product(c, acc):
+            st[c]["spline"] = acc[:, 256 : 256 + UNITS * CHUNKS[c]]
+            for t in range(CHUNKS[c]):
+                mx_group(c, t, st[c]["spline"], [g for group in GROUPS for g in group])
+
         def products(c):
-            st[c]["acc"] = acc_pool.tile([P, 512], F32, name="acc")
-            for t in range(CHUNKS[c]):
-                mx_group(c, t, 0, [-1])
-            for t in range(CHUNKS[c]):
-                mx_group(c, t, 256, [g for group in GROUPS for g in group])
+            acc = acc_pool.tile([P, 512], F32, name="acc")
+            base_product(c, acc)
+            spline_product(c, acc)
 
         def half_tanh(c):
             w = UNITS * CHUNKS[c]
             st[c]["th"] = ep_pool.tile([P, UNITS * CMAX], F32, name="th")
             nc.scalar.activation(
-                out=st[c]["th"][:, :w], in_=st[c]["acc"][:, :w], func=AF.Tanh, scale=0.5
+                out=st[c]["th"][:, :w], in_=st[c]["base"], func=AF.Tanh, scale=0.5
             )
 
         def silu_twice(c):
@@ -321,7 +332,7 @@ def tile_kandense_t_kernel(tc, x, base_weight, spline_weight, out):
                 out=st[c]["s2"][:, :w],
                 in0=st[c]["th"][:, :w],
                 scalar=1.0,
-                in1=st[c]["acc"][:, :w],
+                in1=st[c]["base"],
                 op0=ALU.add,
                 op1=ALU.mult,
             )
@@ -334,7 +345,7 @@ def tile_kandense_t_kernel(tc, x, base_weight, spline_weight, out):
                 out=res[:, :w],
                 in0=st[c]["s2"][:, :w],
                 scalar=0.5,
-                in1=st[c]["acc"][:, 256 : 256 + w],
+                in1=st[c]["spline"],
                 op0=ALU.mult,
                 op1=ALU.add,
             )
@@ -347,6 +358,7 @@ def tile_kandense_t_kernel(tc, x, base_weight, spline_weight, out):
             return 0 <= c < n_chunks
 
         done = [0]
+        last = n_chunks - 1
 
         def quantise_up_to(unit):
             while done[0] < min(unit, len(GROUPS) * n_chunks):
@@ -355,15 +367,15 @@ def tile_kandense_t_kernel(tc, x, base_weight, spline_weight, out):
                 done[0] += 1
 
         def vector_arguments(c):
-            last = CHUNKS[c] - 1
-            work = [(g, t) for g in (0, 1) for t in range(CHUNKS[c])] + [(4, last)]
+            end = CHUNKS[c] - 1
+            work = [(g, t) for g in (0, 1) for t in range(CHUNKS[c])] + [(4, end)]
             work = [(g, t) for g, t in work if (c, g) not in ON_SCALAR]
             if c in WITHOUT_GPSIMD:
                 work = [(3, 0), (2, 0)] + work
             for g, t in work:
                 vector_argument(c, g, t, on_tensor(c) if (g, t) == (1, 0) else 0)
             if c not in WITHOUT_GPSIMD and SHARE < FEAT:
-                vector_argument(c, 3, last, SHARE)
+                vector_argument(c, 3, end, SHARE)
 
         load(0)
         load(1)
@@ -375,12 +387,12 @@ def tile_kandense_t_kernel(tc, x, base_weight, spline_weight, out):
         copy_x(0, 0)
         vector_arguments(0)
 
-        for k in range(n_chunks + 2):
+        for k in range(n_chunks):
             if k == W_PERIOD + 1:
                 products(k - 3)
             if live(k + 4):
                 load(k + 4)
-            settle = live(k - 3) and k <= n_chunks and k != W_PERIOD + 1
+            settle = live(k - 3) and k != W_PERIOD + 1
             if settle:
                 silu_twice(k - 3)
             if live(k + 1) and CHUNKS[k + 1] > 1:
@@ -389,9 +401,8 @@ def tile_kandense_t_kernel(tc, x, base_weight, spline_weight, out):
                 finish(k - 3)
             if live(k + 1):
                 copy_x(k + 1, CHUNKS[k + 1] - 1)
-            quantise_up_to(len(GROUPS) * k - LAG if live(k) else len(GROUPS) * n_chunks)
-            if live(k):
-                quantise_x(k)
+            quantise_up_to(len(GROUPS) * k - LAG)
+            quantise_x(k)
             if live(k + 2):
                 negate(k + 2)
             if k == W_PERIOD:
@@ -425,6 +436,11 @@ def tile_kandense_t_kernel(tc, x, base_weight, spline_weight, out):
                 exp_psum(k, 4)
             if live(k - 2) and k != W_PERIOD:
                 half_tanh(k - 2)
+            if k == last:
+                for c in (k - 1, k):
+                    bank = ab_pool.tile([P, 4, P], F32, name="bank")
+                    base_product(c, bank[:].rearrange("p s m -> p (s m)"))
+                    half_tanh(c)
             if live(k):
                 exp_sbuf(k, 2, 1)
                 exp_sbuf(k, 4, 1)
@@ -435,6 +451,15 @@ def tile_kandense_t_kernel(tc, x, base_weight, spline_weight, out):
             if k == W_PERIOD + 1:
                 silu_twice(k - 3)
                 finish(k - 3)
-            if k >= n_chunks and live(k - 2):
-                silu_twice(k - 2)
-                finish(k - 2)
+        quantise_up_to(len(GROUPS) * last)
+        silu_twice(last - 2)
+        quantise_up_to(len(GROUPS) * last + 1)
+        finish(last - 2)
+        for c in (last - 1, last):
+            silu_twice(c)
+        spline_product(last - 1, acc_pool.tile([P, 512], F32, name="acc"))
+        quantise_up_to(len(GROUPS) * last + 2)
+        finish(last - 1)
+        quantise_up_to(len(GROUPS) * n_chunks)
+        spline_product(last, acc_pool.tile([P, 512], F32, name="acc"))
+        finish(last)

from contextlib import ExitStack

import concourse.mybir as mybir
from concourse.masks import make_identity

FP8X4 = mybir.dt.float8_e4m3fn_x4
BF16 = mybir.dt.bfloat16
F32 = mybir.dt.float32
U32 = mybir.dt.uint32
U8 = mybir.dt.uint8
AF = mybir.ActivationFunctionType
ALU = mybir.AluOpType

P = 128
ROWS, FEAT, UNITS = 6144, 1024, 128
CENTRES = (-1.0, -0.5, 0.0, 0.5, 1.0)
NG = len(CENTRES)
MAPS = 1 + NG
FLOPS = 2 * ROWS * FEAT * UNITS * MAPS

CHUNKS = (1, 1) + (2,) * 22 + (1, 1)
CMAX = 2
GROUPS = ((0, 3), (1, 2), (4,))
SLOT = {-1: 0, 0: 1, 3: 2, 1: 3, 2: 4, 4: 5}
LAG = 1
ON_SCALAR = ((0, 0), (0, 1), (1, 0), (1, 1))
WITHOUT_GPSIMD = (0, 1)
W_PERIOD = 2
SHARE = 768


def tile_kandense_t_kernel(tc, x, base_weight, spline_weight, out):
    nc = tc.nc
    assert sum(CHUNKS) * P == ROWS
    row0 = [P * sum(CHUNKS[:c]) for c in range(len(CHUNKS))]
    n_chunks = len(CHUNKS)

    with ExitStack() as ctx:
        const = ctx.enter_context(tc.tile_pool(name="const", bufs=1))
        xn_pool = ctx.enter_context(tc.tile_pool(name="xn", bufs=4))
        nat_pool = ctx.enter_context(tc.tile_pool(name="nat", bufs=3))
        xg_pool = ctx.enter_context(tc.tile_pool(name="xg", bufs=2))
        arg_pool = ctx.enter_context(tc.tile_pool(name="arg", bufs=2))
        rg_pool = ctx.enter_context(tc.tile_pool(name="rg", bufs=2))
        cd_pool = ctx.enter_context(tc.tile_pool(name="cd", bufs=3))
        ep_pool = ctx.enter_context(tc.tile_pool(name="ep", bufs=3))
        xt_pool = ctx.enter_context(tc.psum_pool(name="xt", bufs=3))
        ab_pool = ctx.enter_context(tc.psum_pool(name="ab", bufs=3))
        acc_pool = ctx.enter_context(tc.psum_pool(name="acc", bufs=2))
        ctx.enter_context(tc.manual_schedule())

        ident = const.tile([P, P], F32, name="ident")
        make_identity(nc, ident[:])
        factor = {}
        for g in (1, 4):
            factor[g] = const.tile([P, P], BF16, name="factor" + str(g))
            nc.vector.tensor_scalar(
                out=factor[g][:],
                in0=ident[:],
                scalar1=-2.0 * CENTRES[g],
                scalar2=None,
                op0=ALU.mult,
            )
        shift = const.tile([P, 8], F32, name="shift")
        for g in range(NG):
            nc.vector.memset(shift[:, g : g + 1], -5.0 * CENTRES[g] * CENTRES[g])
        nc.vector.memset(shift[:, 5:6], 0.0)
        for g in (0, 1):
            nc.vector.memset(shift[:, 6 + g : 7 + g], -CENTRES[g])
        warm_out = const.tile([P, 1], F32, name="warm_out")
        nc.scalar.activation(out=warm_out[:], in_=shift[:, 5:6], func=AF.Exp)

        wb_raw = const.tile([P, 4, 2 * UNITS], BF16, name="wb_raw")
        ws_raw = const.tile([P, 4, 2 * UNITS * 8], BF16, name="ws_raw")
        w_grouped = const.tile([P, MAPS, 2, UNITS, 4], BF16, name="w_grouped", align_bytes=64)
        w_codes = const.tile([P, MAPS * 2 * UNITS], U32, name="w_codes", align_bytes=64)
        w_scales = const.tile([P, MAPS * 2 * UNITS], U8, name="w_scales", align_bytes=64)

        st = [dict() for c in range(n_chunks)]

        def load(c):
            n = CHUNKS[c]
            xn = xn_pool.tile([P, CMAX, FEAT], BF16, name="xn")
            st[c]["xn"] = xn
            nc.sync.dma_start(
                out=xn[:, :n, :],
                in_=x[row0[c] : row0[c] + P * n, :].rearrange("(p t) k -> p t k", t=n),
            )

        def load_weights():
            nc.sync.dma_start(
                out=wb_raw[:], in_=base_weight.rearrange("(a p e) c -> p a (e c)", a=4, p=P, e=2)
            )
            nc.sync.dma_start(
                out=ws_raw[:],
                in_=spline_weight.rearrange("(a p e) c s -> p a (e c s)", a=4, p=P, e=2),
            )

        def regroup_weights():
            for m in range(MAPS):
                if m == 0:
                    src = wb_raw[:].rearrange("p a (e c) -> p (a e) c", e=2)
                else:
                    src = ws_raw[:].rearrange("p a (e c s) -> p (a e) c s", e=2, s=8)[:, :, :, m - 1]
                nc.vector.tensor_copy(
                    out=w_grouped[:, m], in_=src.rearrange("p (h t) c -> p h c t", h=2)
                )

        def quantise_weights():
            flat = w_grouped[:].rearrange("p m h c t -> p (m h c t)")
            for lo, hi in ((0, 1024), (1024, 1536)):
                nc.vector.quantize_mx(
                    out=w_codes[:, lo:hi].bitcast(FP8X4),
                    scales=w_scales[:, lo:hi],
                    in_=flat[:, 4 * lo : 4 * hi],
                )

        def negate(c):
            if CHUNKS[c] == 1:
                return
            st[c]["neg"] = nat_pool.tile([P, 8, P], F32, name="neg")
            nc.vector.tensor_scalar(
                out=st[c]["neg"][:].rearrange("q (j e) p -> q j e p", e=2),
                in0=st[c]["xn"][:, 0, :].rearrange("q (j p e) -> q j e p", j=4, e=2),
                scalar1=-1.0,
                scalar2=None,
                op0=ALU.mult,
            )

        def square(c):
            if CHUNKS[c] == 1:
                return
            st[c]["sq"] = nat_pool.tile([P, 8, P], F32, name="sq")
            neg = st[c]["neg"][:].rearrange("q b p -> q (b p)")
            nc.gpsimd.tensor_tensor(
                out=st[c]["sq"][:].rearrange("q b p -> q (b p)"), in0=neg, in1=neg, op=ALU.mult
            )

        def transposes(c):
            words = st[c]["xn"][:].bitcast(F32)
            st[c]["xt"] = []
            for t in range(CHUNKS[c]):
                xt = xt_pool.tile([P, 256, 2], F32, name="xt")
                st[c]["xt"].append(xt)
                for j in range(4):
                    h, u = divmod(j, 2)
                    nc.tensor.transpose(
                        xt[:, P * h : P * h + P, u], words[:, t, P * j : P * j + P], ident[:]
                    )

        def copy_x(c, t):
            if "xg" not in st[c]:
                st[c]["xg"] = xg_pool.tile([P, CMAX * FEAT], BF16, name="xg", align_bytes=64)
            nc.vector.tensor_copy(
                out=st[c]["xg"][:].bitcast(F32)[:, 512 * t : 512 * t + 512],
                in_=st[c]["xt"][t][:].rearrange("p m u -> p (m u)"),
            )

        def quantise(c, slot, maps, src):
            n = CHUNKS[c]
            words = slice(256 * n * slot, 256 * n * (slot + maps))
            nc.vector.quantize_mx(
                out=st[c]["codes"][:, words].bitcast(FP8X4),
                scales=st[c]["scales"][:, words],
                in_=src[:, : FEAT * n * maps],
            )

        def quantise_x(c):
            st[c]["codes"] = cd_pool.tile([P, MAPS * CMAX * 256], U32, name="codes", align_bytes=64)
            st[c]["scales"] = cd_pool.tile([P, MAPS * CMAX * 256], U8, name="scales", align_bytes=64)
            quantise(c, 0, 1, st[c]["xg"])

        def argument_tile(c, g):
            if ("arg", g) not in st[c]:
                width = CMAX * FEAT if g in (0, 1) else FEAT
                st[c]["arg", g] = arg_pool.tile([P, width], F32, name="arg" + str(g))
            return st[c]["arg", g]

        def argument(c, g, t):
            lo = FEAT * t if g in (0, 1) else 0
            return argument_tile(c, g)[:, lo : lo + FEAT]

        def on_tensor(c):
            return 512 if CHUNKS[c] > 1 else 0

        def by_transposes(c, g, h):
            if g == 4:
                return 2 if h == 0 and c % 5 in (1, 3) else 0
            return 1 if g == 3 else 0

        def vector_argument(c, g, t, lo=0):
            nc.vector.scalar_tensor_tensor(
                out=argument(c, g, t)[:, lo:],
                in0=st[c]["xt"][t][:].rearrange("p m u -> p (m u)").bitcast(BF16)[:, lo:],
                scalar=2.0 * CENTRES[g],
                in1=st[c]["xg"][:, FEAT * t + lo : FEAT * t + FEAT],
                op0=ALU.subtract,
                op1=ALU.mult,
            )

        def last_xg(c):
            t = CHUNKS[c] - 1
            return st[c]["xg"][:, FEAT * t : FEAT * t + FEAT]

        def gpsimd_square(c):
            arg = argument(c, 2, CHUNKS[c] - 1)
            nc.gpsimd.tensor_tensor(out=arg, in0=last_xg(c), in1=last_xg(c), op=ALU.mult)

        def gpsimd_difference(c):
            t = CHUNKS[c] - 1
            nc.gpsimd.tensor_tensor(
                out=argument(c, 3, t)[:, :SHARE],
                in0=argument(c, 2, t)[:, :SHARE],
                in1=last_xg(c)[:, :SHARE],
                op=ALU.subtract,
            )

        def tensor_argument(c, g, halves=(0, 1)):
            if CHUNKS[c] == 1:
                return
            st[c]["bank", g] = []
            for h in halves:
                bank = ab_pool.tile([P, 4, P], F32, name="bank")
                st[c]["bank", g].append(bank)
                for s in range(4):
                    sq, neg = st[c]["sq"][:, 4 * h + s, :], st[c]["neg"][:, 4 * h + s, :]
                    nc.tensor.matmul(
                        bank[:, s, :], sq, ident[:], start=True, stop=(g == 2), is_transpose=True
                    )
                    repeat = by_transposes(c, g, h)
                    for i in range(repeat):
                        nc.tensor.matmul(
                            bank[:, s, :], neg, ident[:], start=False, stop=(i == repeat - 1), is_transpose=True
                        )
                    if g in (1, 4) and repeat == 0:
                        nc.tensor.matmul(
                            bank[:, s, :],
                            factor[g][:],
                            st[c]["xg"][:, 512 * h : 512 * h + 512].rearrange(
                                "p (m s) -> p m s", s=4
                            )[:, :, s],
                            start=False,
                            stop=True,
                        )

        def rbf(c, g):
            for i, group in enumerate(GROUPS):
                if g in group:
                    if ("rg", i) not in st[c]:
                        st[c]["rg", i] = rg_pool.tile(
                            [P, len(group) * CMAX * FEAT], BF16, name="rg" + str(i), align_bytes=64
                        )
                    n = FEAT * CHUNKS[c]
                    lo = n * group.index(g)
                    return st[c]["rg", i][:, lo : lo + n]

        def exp_sbuf(c, g, first=0, skip=0):
            n = FEAT * CHUNKS[c]
            lo = FEAT * first if CHUNKS[c] > 1 else 0
            complete = (c, g) in ON_SCALAR
            if complete:
                arg = argument_tile(c, g)
                nc.scalar.activation(
                    out=arg[:, :n],
                    in_=st[c]["xg"][:, :n],
                    func=AF.Square,
                    bias=shift[:, 6 + g : 7 + g],
                )
            nc.scalar.activation(
                out=rbf(c, g)[:, lo + skip : n],
                in_=st[c]["arg", g][:, skip : n - lo],
                func=AF.Exp,
                scale=-5.0,
                bias=shift[:, 5:6] if complete else shift[:, g : g + 1],
            )

        def exp_psum(c, g):
            if CHUNKS[c] == 1:
                return
            for h, bank in enumerate(st[c]["bank", g]):
                nc.scalar.activation(
                    out=rbf(c, g)[:, 512 * h : 512 * h + 512].rearrange("p (m s) -> p m s", s=4),
                    in_=bank[:].rearrange("p s m -> p m s"),
                    func=AF.Exp,
                    scale=-5.0,
                    bias=shift[:, g : g + 1],
                )

        def mx_group(c, t, acc, centres):
            codes, scales, n = st[c]["codes"], st[c]["scales"], CHUNKS[c]
            steps = [(g, h) for g in centres for h in range(2)]
            for i, (g, h) in enumerate(steps):
                col = 256 * n * SLOT[g] + P * (2 * t + h)
                a = slice(col, col + P)
                b = slice(P * (2 * (g + 1) + h), P * (2 * (g + 1) + h) + P)
                nc.tensor.matmul_mx(
                    out=acc[:, P * t : P * t + P],
                    lhsT=codes[:, a].bitcast(FP8X4),
                    lhsT_scale=scales[:, a],
                    rhs=w_codes[:, b].bitcast(FP8X4),
                    rhs_scale=w_scales[:, b],
                    start=(i == 0),
                    stop=(i == len(steps) - 1),
                )

        def base_product(c, acc):
            st[c]["base"] = acc[:, : UNITS * CHUNKS[c]]
            for t in range(CHUNKS[c]):
                mx_group(c, t, st[c]["base"], [-1])

        def spline_product(c, acc):
            st[c]["spline"] = acc[:, 256 : 256 + UNITS * CHUNKS[c]]
            for t in range(CHUNKS[c]):
                mx_group(c, t, st[c]["spline"], [g for group in GROUPS for g in group])

        def products(c):
            acc = acc_pool.tile([P, 512], F32, name="acc")
            base_product(c, acc)
            spline_product(c, acc)

        def half_tanh(c):
            w = UNITS * CHUNKS[c]
            st[c]["th"] = ep_pool.tile([P, UNITS * CMAX], F32, name="th")
            nc.scalar.activation(
                out=st[c]["th"][:, :w], in_=st[c]["base"], func=AF.Tanh, scale=0.5
            )

        def silu_twice(c):
            w = UNITS * CHUNKS[c]
            st[c]["s2"] = ep_pool.tile([P, UNITS * CMAX], F32, name="s2")
            nc.vector.scalar_tensor_tensor(
                out=st[c]["s2"][:, :w],
                in0=st[c]["th"][:, :w],
                scalar=1.0,
                in1=st[c]["base"],
                op0=ALU.add,
                op1=ALU.mult,
            )

        def finish(c):
            n = CHUNKS[c]
            w = UNITS * n
            res = ep_pool.tile([P, UNITS * CMAX], F32, name="res")
            nc.vector.scalar_tensor_tensor(
                out=res[:, :w],
                in0=st[c]["s2"][:, :w],
                scalar=0.5,
                in1=st[c]["spline"],
                op0=ALU.mult,
                op1=ALU.add,
            )
            nc.sync.dma_start(
                out=out[row0[c] : row0[c] + P * n, :].rearrange("(p t) u -> p (t u)", t=n),
                in_=res[:, :w],
            )

        def live(c):
            return 0 <= c < n_chunks

        done = [0]
        last = n_chunks - 1

        def quantise_up_to(unit):
            while done[0] < min(unit, len(GROUPS) * n_chunks):
                c, i = divmod(done[0], len(GROUPS))
                quantise(c, SLOT[GROUPS[i][0]], len(GROUPS[i]), st[c]["rg", i])
                done[0] += 1

        def vector_arguments(c):
            end = CHUNKS[c] - 1
            work = [(g, t) for g in (0, 1) for t in range(CHUNKS[c])] + [(4, end)]
            work = [(g, t) for g, t in work if (c, g) not in ON_SCALAR]
            if c in WITHOUT_GPSIMD:
                work = [(3, 0), (2, 0)] + work
            for g, t in work:
                vector_argument(c, g, t, on_tensor(c) if (g, t) == (1, 0) else 0)
            if c not in WITHOUT_GPSIMD and SHARE < FEAT:
                vector_argument(c, 3, end, SHARE)

        load(0)
        load(1)
        load(2)
        load_weights()
        load(3)
        transposes(0)
        transposes(1)
        copy_x(0, 0)
        vector_arguments(0)

        for k in range(n_chunks):
            if k == W_PERIOD + 1:
                products(k - 3)
            if live(k + 4):
                load(k + 4)
            settle = live(k - 3) and k != W_PERIOD + 1
            if settle:
                silu_twice(k - 3)
            if live(k + 1) and CHUNKS[k + 1] > 1:
                copy_x(k + 1, 0)
            if settle:
                finish(k - 3)
            if live(k + 1):
                copy_x(k + 1, CHUNKS[k + 1] - 1)
            quantise_up_to(len(GROUPS) * k - LAG)
            quantise_x(k)
            if live(k + 2):
                negate(k + 2)
            if k == W_PERIOD:
                regroup_weights()
                quantise_weights()
            if live(k + 2):
                square(k + 2)
            if live(k + 1) and k + 1 not in WITHOUT_GPSIMD:
                gpsimd_square(k + 1)
                gpsimd_difference(k + 1)
            if live(k):
                exp_psum(k, 3)
                exp_sbuf(k, 0)
                tensor_argument(k, 2)
                exp_psum(k, 2)
                exp_sbuf(k, 3, 1)
            if live(k) and on_tensor(k) > 0:
                tensor_argument(k, 1, (0,))
            if live(k - 2) and k != W_PERIOD:
                products(k - 2)
            if live(k):
                tensor_argument(k, 4)
            if live(k + 1):
                tensor_argument(k + 1, 3)
            if live(k + 2):
                transposes(k + 2)
            if live(k):
                if on_tensor(k) > 0:
                    exp_psum(k, 1)
                exp_sbuf(k, 1, 0, on_tensor(k))
                exp_psum(k, 4)
            if live(k - 2) and k != W_PERIOD:
                half_tanh(k - 2)
            if k == last:
                for c in (k - 1, k):
                    bank = ab_pool.tile([P, 4, P], F32, name="bank")
                    base_product(c, bank[:].rearrange("p s m -> p (s m)"))
                    half_tanh(c)
            if live(k):
                exp_sbuf(k, 2, 1)
                exp_sbuf(k, 4, 1)
            if k == W_PERIOD + 1:
                half_tanh(k - 3)
            if live(k + 1):
                vector_arguments(k + 1)
            if k == W_PERIOD + 1:
                silu_twice(k - 3)
                finish(k - 3)
        quantise_up_to(len(GROUPS) * last)
        silu_twice(last - 2)
        quantise_up_to(len(GROUPS) * last + 1)
        finish(last - 2)
        for c in (last - 1, last):
            silu_twice(c)
        spline_product(last - 1, acc_pool.tile([P, 512], F32, name="acc"))
        quantise_up_to(len(GROUPS) * last + 2)
        finish(last - 1)
        quantise_up_to(len(GROUPS) * n_chunks)
        spline_product(last, acc_pool.tile([P, 512], F32, name="acc"))
        finish(last)
